import numpy as np
import ml_dtypes


def mxq(x, axis, fmt="e4m3"):
    dtype, down = {"e4m3": (ml_dtypes.float8_e4m3fn, 7), "e5m2": (ml_dtypes.float8_e5m2, 14)}[fmt]
    v = np.moveaxis(np.asarray(x, np.float32).astype(ml_dtypes.bfloat16).astype(np.float64), axis, -1)
    blocks = v.reshape(v.shape[:-1] + (-1, 32))
    amax = np.abs(blocks).max(-1, keepdims=True)
    byte = np.maximum(np.where(amax > 0, np.frexp(amax)[1] - 1 + 127, 0) - down, 1)
    scale = np.exp2(byte - 127.0)
    codes = (blocks / scale).astype(np.float32).astype(dtype).astype(np.float64)
    return np.moveaxis((codes * scale).reshape(v.shape), -1, axis)


WIDE = False


def mx_kscale(k):
    if not WIDE:
        return np.ones(k)
    levels = np.array([10, -10, 5, -5, 0])
    if k % 512:
        return np.exp2(np.random.permutation(np.resize(levels, k // 32))).repeat(32)
    a = np.empty((k // 512, 16))
    for p in range(k // 512):
        a[p, :8] = np.random.permutation(np.resize(levels, 8))
        for g in range(8):
            far = levels[np.abs(levels - a[p, g]) >= 10]
            a[p, g + 8] = far[np.random.randint(len(far))]
    return np.exp2(a.ravel()).repeat(32)


BF16 = ml_dtypes.bfloat16


def bf(x):
    return np.asarray(x, np.float32).astype(BF16)


def f64(x):
    return np.asarray(x).astype(np.float64)


B, N, P, C, HID, NB, E, MAXLEN = 2, 64, 3, 256, 128, 63, 512, 2056
EPS = 1e-5


def setup_inputs():
    s, t = mx_kscale(E), mx_kscale(E)
    return {"h1": bf(np.maximum(np.random.standard_normal((B, N, N, E)), 0.0) * s),
            "edge_mask": bf(np.random.random((B, N, N)) > 0.15),
            "W2": bf(np.random.standard_normal((E, E)) * 1.4 / np.sqrt(E) / s[:, None] * t),
            "b2": bf(np.random.standard_normal(E) * 0.3 * t),
            "W3": bf(np.random.standard_normal((E, E)) * 1.4 / np.sqrt(E) / t[:, None]),
            "b3": bf(np.random.standard_normal(E) * 0.3),
            "ln_g": bf(1.0 + 0.2 * np.random.standard_normal(E)),
            "ln_b": bf(0.2 * np.random.standard_normal(E))}


def reference(h1, edge_mask, W2, b2, W3, b3, ln_g, ln_b):
    h = np.maximum((mxq(f64(h1), 3, "e4m3") @ mxq(f64(W2), 0, "e4m3")) + f64(b2), 0.0)
    h = (mxq(h, 3, "e4m3") @ mxq(f64(W3), 0, "e4m3")) + f64(b3)
    mu = h.mean(-1, keepdims=True)
    var = h.var(-1, keepdims=True)
    h = (h - mu) / np.sqrt(var + EPS) * f64(ln_g) + f64(ln_b)
    return h * f64(edge_mask)[..., None]

@@ -1,0 +1,306 @@
+from contextlib import ExitStack
+
+import concourse.mybir as mybir
+from concourse.masks import make_identity
+
+F32 = mybir.dt.float32
+BF16 = mybir.dt.bfloat16
+U32 = mybir.dt.uint32
+U8 = mybir.dt.uint8
+FP8X4 = mybir.dt.float8_e4m3fn_x4
+ALU = mybir.AluOpType
+ACT = mybir.ActivationFunctionType
+
+P = 128
+PACK = 4
+E = 512
+ROWS = 2 * 64 * 64
+ROWS_PER_PARTITION = ROWS // P
+TILES_PER_CHUNK = 4
+CHUNK_COLS = TILES_PER_CHUNK * P
+N_CHUNKS = ROWS_PER_PARTITION // TILES_PER_CHUNK
+WORDS = E // 2
+EPS = 1e-5
+
+FLOPS = 2 * 2 * ROWS * E * E
+
+
+def tile_edgefeaturenet_pb_t_kernel(tc, h1, edge_mask, W2, b2, W3, b3, ln_g, ln_b, out):
+    nc = tc.nc
+    h1_rows = h1.flatten_outer_dims().rearrange("(p t) k -> p (t k)", t=ROWS_PER_PARTITION)
+    out_rows = out.flatten_outer_dims().rearrange("(p t) f -> p (t f)", t=ROWS_PER_PARTITION)
+    mask_rows = edge_mask.rearrange("b n m -> (b n m)").rearrange("(p t) -> p t", t=ROWS_PER_PARTITION)
+
+    with ExitStack() as ctx:
+        keep = ctx.enter_context(tc.tile_pool(name="keep", bufs=1))
+        two = ctx.enter_context(tc.tile_pool(name="two", bufs=2))
+        three = ctx.enter_context(tc.tile_pool(name="three", bufs=3))
+        four = ctx.enter_context(tc.tile_pool(name="four", bufs=4))
+        psum_t = ctx.enter_context(tc.psum_pool(name="psum_t", bufs=2))
+        psum_1 = ctx.enter_context(tc.psum_pool(name="psum_1", bufs=2))
+        psum_keep = ctx.enter_context(tc.psum_pool(name="psum_keep", bufs=1))
+        psum_2 = ctx.enter_context(tc.psum_pool(name="psum_2", bufs=3))
+        ctx.enter_context(tc.manual_schedule())
+
+        live = {}
+
+        def chunk_cols(c):
+            return slice(c * TILES_PER_CHUNK * E, (c + 1) * TILES_PER_CHUNK * E)
+
+        def load(c):
+            x = three.tile([P, TILES_PER_CHUNK * E], BF16, name="x")
+            nc.sync.dma_start(out=x[:], in_=h1_rows[:, chunk_cols(c)])
+            live["x", c] = x
+
+        def mask_the_shift(c):
+            masked_shift = three.tile([P, TILES_PER_CHUNK, E], F32, name="masked_shift")
+            for j in range(TILES_PER_CHUNK):
+                t = c * TILES_PER_CHUNK + j
+                nc.gpsimd.tensor_scalar(
+                    out=masked_shift[:, j, :],
+                    in0=shift_all[:],
+                    scalar1=mask_f32[:, t : t + 1],
+                    scalar2=0.0,
+                    op0=ALU.mult,
+                    op1=ALU.add,
+                )
+            live["masked_shift", c] = masked_shift
+
+        def flip(c):
+            x_words = live["x", c][:].bitcast(F32)
+            for half in range(2):
+                flipped = psum_t.tile([P, 2, 2 * P], F32, name="flipped")
+                for jj in range(2):
+                    j = 2 * half + jj
+                    for u in range(2):
+                        nc.tensor.transpose(
+                            flipped[:, u, jj * P : (jj + 1) * P],
+                            x_words[:, j * WORDS + u : (j + 1) * WORDS : 2],
+                            ident[:],
+                        )
+                live["flipped", c, half] = flipped
+
+        def group_x(c):
+            x_grouped = two.tile([P, CHUNK_COLS * PACK], BF16, align_bytes=64, name="x_grouped")
+            x_grouped_words = x_grouped[:].bitcast(F32).rearrange("q (n u) -> q n u", u=2)
+            for half in range(2):
+                nc.scalar.copy(
+                    out=x_grouped_words[:, half * 2 * P : (half + 1) * 2 * P, :],
+                    in_=live["flipped", c, half][:].rearrange("q u n -> q n u"),
+                )
+            live["x_grouped", c] = x_grouped
+
+        def quantise_x(c):
+            x_codes = four.tile([P, CHUNK_COLS], U32, align_bytes=64, name="x_codes")
+            x_scales = four.tile([P, CHUNK_COLS], U8, align_bytes=64, name="x_scales")
+            nc.vector.quantize_mx(
+                out=x_codes[:].bitcast(FP8X4), scales=x_scales[:], in_=live["x_grouped", c][:]
+            )
+            live["x_codes", c] = x_codes
+            live["x_scales", c] = x_scales
+
+        def layer1_pass(c, m):
+            acc1 = psum_1.tile([P, CHUNK_COLS], F32, name="acc1")
+            nc.tensor.matmul_mx(
+                out=acc1[:],
+                lhsT=w2_codes[:, m * P : (m + 1) * P].bitcast(FP8X4),
+                lhsT_scale=w2_scales[:, m * P : (m + 1) * P],
+                rhs=live["x_codes", c][:].bitcast(FP8X4),
+                rhs_scale=live["x_scales", c][:],
+                start=True,
+                stop=True,
+            )
+            live["acc1", c, m] = acc1
+
+        def relu_and_group_h(c):
+            h_planes = two.tile([P, PACK, CHUNK_COLS], BF16, name="h_planes")
+            for m in range(PACK):
+                nc.scalar.activation(
+                    out=h_planes[:, m, :],
+                    in_=live["acc1", c, m][:],
+                    func=ACT.Relu,
+                    bias=b2_f32[:, m : m + 1],
+                    scale=1.0,
+                )
+            h_grouped = two.tile([P, CHUNK_COLS, PACK], BF16, align_bytes=64, name="h_grouped")
+            nc.scalar.copy(
+                out=h_grouped[:].rearrange("p (n i) t -> p n t i", i=4),
+                in_=h_planes[:].rearrange("p t (n i) -> p n t i", i=4),
+            )
+            live["h_grouped", c] = h_grouped
+
+        def quantise_h(c):
+            h_codes = three.tile([P, CHUNK_COLS], U32, align_bytes=64, name="h_codes")
+            h_scales = three.tile([P, CHUNK_COLS], U8, align_bytes=64, name="h_scales")
+            nc.vector.quantize_mx(
+                out=h_codes[:].bitcast(FP8X4),
+                scales=h_scales[:],
+                in_=live["h_grouped", c][:].rearrange("p n t -> p (n t)"),
+            )
+            live["h_codes", c] = h_codes
+            live["h_scales", c] = h_scales
+
+        def layer2_pass(c, j):
+            acc2 = psum_2.tile([P, E], F32, name="acc2")
+            nc.tensor.matmul_mx(
+                out=acc2[:],
+                lhsT=live["h_codes", c][:, j * P : (j + 1) * P].bitcast(FP8X4),
+                lhsT_scale=live["h_scales", c][:, j * P : (j + 1) * P],
+                rhs=w3_codes[:].bitcast(FP8X4),
+                rhs_scale=w3_scales[:],
+                start=True,
+                stop=True,
+            )
+            live["acc2", c, j] = acc2
+
+        def add_bias_and_mean(c):
+            y = two.tile([P, TILES_PER_CHUNK, E], F32, name="y")
+            row_sum = three.tile([P, TILES_PER_CHUNK], F32, name="row_sum")
+            for j in range(TILES_PER_CHUNK):
+                nc.vector.scalar_tensor_tensor(
+                    out=y[:, j, :],
+                    in0=live["acc2", c, j][:],
+                    scalar=1.0,
+                    in1=b3_all[:],
+                    op0=ALU.mult,
+                    op1=ALU.add,
+                    accum_out=row_sum[:, j : j + 1],
+                )
+            neg_mean = three.tile([P, TILES_PER_CHUNK], F32, name="neg_mean")
+            nc.vector.tensor_scalar(
+                out=neg_mean[:], in0=row_sum[:], scalar1=-1.0 / E, scalar2=None, op0=ALU.mult
+            )
+            live["y", c] = y
+            live["neg_mean", c] = neg_mean
+
+        def deviation(c):
+            square_sum = three.tile([P, TILES_PER_CHUNK], F32, name="square_sum")
+            for j in range(TILES_PER_CHUNK):
+                squares = two.tile([P, E], F32, name="squares")
+                nc.scalar.activation(
+                    out=squares[:],
+                    in_=live["y", c][:, j, :],
+                    func=ACT.Square,
+                    bias=live["neg_mean", c][:, j : j + 1],
+                    scale=1.0,
+                    accum_out=square_sum[:, j : j + 1],
+                )
+            std = three.tile([P, TILES_PER_CHUNK], F32, name="std")
+            nc.scalar.activation(out=std[:], in_=square_sum[:], func=ACT.Sqrt, bias=eps[:, 0:1], scale=1.0 / E)
+            live["std", c] = std
+
+        def centre_and_gain(c):
+            gained = three.tile([P, TILES_PER_CHUNK, E], F32, name="gained")
+            for j in range(TILES_PER_CHUNK):
+                nc.vector.scalar_tensor_tensor(
+                    out=gained[:, j, :],
+                    in0=live["y", c][:, j, :],
+                    scalar=live["neg_mean", c][:, j : j + 1],
+                    in1=gain_all[:],
+                    op0=ALU.add,
+                    op1=ALU.mult,
+                )
+            live["gained", c] = gained
+
+        def scale_shift_store(c):
+            inv_std = three.tile([P, TILES_PER_CHUNK], F32, name="inv_std")
+            nc.vector.reciprocal(out=inv_std[:], in_=live["std", c][:])
+            row_scale = three.tile([P, TILES_PER_CHUNK], F32, name="row_scale")
+            nc.vector.tensor_mul(
+                out=row_scale[:],
+                in0=inv_std[:],
+                in1=mask_f32[:, c * TILES_PER_CHUNK : (c + 1) * TILES_PER_CHUNK],
+            )
+            result = three.tile([P, TILES_PER_CHUNK, E], F32, name="result")
+            for j in range(TILES_PER_CHUNK):
+                nc.vector.scalar_tensor_tensor(
+                    out=result[:, j, :],
+                    in0=live["gained", c][:, j, :],
+                    scalar=row_scale[:, j : j + 1],
+                    in1=live["masked_shift", c][:, j, :],
+                    op0=ALU.mult,
+                    op1=ALU.add,
+                )
+                if j % 2 == 1:
+                    first = (c * TILES_PER_CHUNK + j - 1) * E
+                    nc.sync.dma_start(
+                        out=out_rows[:, first : first + 2 * E],
+                        in_=result[:, j - 1 : j + 1, :].rearrange("p j f -> p (j f)"),
+                    )
+
+        def when_in_range(step, c):
+            if 0 <= c < N_CHUNKS:
+                step(c)
+
+        load(0)
+        load(1)
+        w2_raw = keep.tile([P, PACK, E], BF16)
+        nc.scalar.dma_start(out=w2_raw[:], in_=W2.rearrange("(q t) n -> q t n", t=PACK))
+        w3_raw = keep.tile([P, PACK, E], BF16)
+        nc.scalar.dma_start(out=w3_raw[:], in_=W3.rearrange("(p t) n -> p t n", t=PACK))
+        b2_bf = keep.tile([P, PACK], BF16)
+        nc.scalar.dma_start(out=b2_bf[:], in_=b2.rearrange("(r m) -> r m", m=PACK))
+        mask_bf = keep.tile([P, ROWS_PER_PARTITION], BF16)
+        nc.scalar.dma_start(out=mask_bf[:], in_=mask_rows)
+        shift_all = keep.tile([P, E], BF16)
+        nc.scalar.dma_start(out=shift_all[:], in_=ln_b.partition_broadcast(P))
+        b3_all = keep.tile([P, E], BF16)
+        nc.scalar.dma_start(out=b3_all[:], in_=b3.partition_broadcast(P))
+        ones = keep.tile([P, P], BF16)
+        nc.vector.memset(ones[:], 1.0)
+        gain_row = keep.tile([P, E], BF16)
+        nc.vector.memset(gain_row[:], 0.0)
+        nc.scalar.dma_start(out=gain_row[0:1, :], in_=ln_g.rearrange("(o f) -> o f", o=1))
+        gain_all = psum_keep.tile([P, E], F32)
+        nc.tensor.matmul(out=gain_all[:], lhsT=ones[:], rhs=gain_row[:], start=True, stop=True)
+
+        ident = keep.tile([P, P], F32)
+        make_identity(nc, ident[:])
+        eps = keep.tile([P, 1], F32)
+        nc.vector.memset(eps[:], EPS)
+        table_warmer = keep.tile([P, 1], F32)
+        nc.scalar.activation(out=table_warmer[:], in_=eps[:], func=ACT.Sqrt)
+
+        w2_grouped = keep.tile([P, E, PACK], BF16, align_bytes=64)
+        nc.vector.tensor_copy(
+            out=w2_grouped[:].rearrange("q (m r) t -> q m r t", m=PACK),
+            in_=w2_raw[:].rearrange("q t (r m) -> q m r t", m=PACK),
+        )
+        w3_grouped = keep.tile([P, E, PACK], BF16, align_bytes=64)
+        nc.vector.tensor_copy(out=w3_grouped[:], in_=w3_raw[:].rearrange("p t n -> p n t"))
+        w2_codes = keep.tile([P, E], U32, align_bytes=64)
+        w2_scales = keep.tile([P, E], U8, align_bytes=64)
+        nc.vector.quantize_mx(
+            out=w2_codes[:].bitcast(FP8X4),
+            scales=w2_scales[:],
+            in_=w2_grouped[:].rearrange("q n t -> q (n t)"),
+        )
+        w3_codes = keep.tile([P, E], U32, align_bytes=64)
+        w3_scales = keep.tile([P, E], U8, align_bytes=64)
+        nc.vector.quantize_mx(
+            out=w3_codes[:].bitcast(FP8X4),
+            scales=w3_scales[:],
+            in_=w3_grouped[:].rearrange("p n t -> p (n t)"),
+        )
+        b2_f32 = keep.tile([P, PACK], F32)
+        nc.vector.tensor_copy(out=b2_f32[:], in_=b2_bf[:])
+        mask_f32 = keep.tile([P, ROWS_PER_PARTITION], F32)
+        nc.vector.tensor_copy(out=mask_f32[:], in_=mask_bf[:])
+
+        for i in range(-3, N_CHUNKS + 1):
+            when_in_range(add_bias_and_mean, i)
+            when_in_range(scale_shift_store, i - 1)
+            when_in_range(relu_and_group_h, i + 1)
+            when_in_range(quantise_h, i + 1)
+            when_in_range(flip, i + 3)
+            when_in_range(group_x, i + 3)
+            when_in_range(deviation, i)
+            when_in_range(centre_and_gain, i)
+            when_in_range(quantise_x, i + 3)
+            for q in range(PACK):
+                if 0 <= i + 1 < N_CHUNKS:
+                    layer2_pass(i + 1, q)
+                if 0 <= i + 2 < N_CHUNKS:
+                    layer1_pass(i + 2, q)
+            when_in_range(mask_the_shift, i + 2)
+            when_in_range(load, i + 5)

@@ -16,11 +16,13 @@ PACK = 4
 E = 512
 ROWS = 2 * 64 * 64
 ROWS_PER_PARTITION = ROWS // P
-TILES_PER_CHUNK = 4
-CHUNK_COLS = TILES_PER_CHUNK * P
-N_CHUNKS = ROWS_PER_PARTITION // TILES_PER_CHUNK
 WORDS = E // 2
 EPS = 1e-5
+GAIN_ROUND = -2
+GPSIMD_TILES = 2
+WIDTHS = [1, 1, 2] + [4] * 14 + [2, 1, 1]
+N_CHUNKS = len(WIDTHS)
+FIRST = [sum(WIDTHS[:c]) for c in range(N_CHUNKS)]
 
 FLOPS = 2 * 2 * ROWS * E * E
 
@@ -36,63 +38,53 @@ def tile_edgefeaturenet_pb_t_kernel(tc, h1, edge_mask, W2, b2, W3, b3, ln_g, ln_
         two = ctx.enter_context(tc.tile_pool(name="two", bufs=2))
         three = ctx.enter_context(tc.tile_pool(name="three", bufs=3))
         four = ctx.enter_context(tc.tile_pool(name="four", bufs=4))
-        psum_t = ctx.enter_context(tc.psum_pool(name="psum_t", bufs=2))
+        six = ctx.enter_context(tc.tile_pool(name="six", bufs=6))
+        psum_t = ctx.enter_context(tc.psum_pool(name="psum_t", bufs=1))
         psum_1 = ctx.enter_context(tc.psum_pool(name="psum_1", bufs=2))
+        psum_2 = ctx.enter_context(tc.psum_pool(name="psum_2", bufs=2))
+        psum_s = ctx.enter_context(tc.psum_pool(name="psum_s", bufs=2))
         psum_keep = ctx.enter_context(tc.psum_pool(name="psum_keep", bufs=1))
-        psum_2 = ctx.enter_context(tc.psum_pool(name="psum_2", bufs=3))
         ctx.enter_context(tc.manual_schedule())
 
         live = {}
 
-        def chunk_cols(c):
-            return slice(c * TILES_PER_CHUNK * E, (c + 1) * TILES_PER_CHUNK * E)
+        def shift_is_gpsimds(c, j):
+            return gain_is_gpsimds(c, j)
+
+        def gain_is_gpsimds(c, j):
+            return WIDTHS[c] == PACK and j >= PACK - GPSIMD_TILES
 
         def load(c):
-            x = three.tile([P, TILES_PER_CHUNK * E], BF16, name="x")
-            nc.sync.dma_start(out=x[:], in_=h1_rows[:, chunk_cols(c)])
+            x = three.tile([P, WIDTHS[c] * E], BF16, name="x")
+            nc.sync.dma_start(out=x[:], in_=h1_rows[:, FIRST[c] * E : (FIRST[c] + WIDTHS[c]) * E])
             live["x", c] = x
 
-        def mask_the_shift(c):
-            masked_shift = three.tile([P, TILES_PER_CHUNK, E], F32, name="masked_shift")
-            for j in range(TILES_PER_CHUNK):
-                t = c * TILES_PER_CHUNK + j
-                nc.gpsimd.tensor_scalar(
-                    out=masked_shift[:, j, :],
-                    in0=shift_all[:],
-                    scalar1=mask_f32[:, t : t + 1],
-                    scalar2=0.0,
-                    op0=ALU.mult,
-                    op1=ALU.add,
-                )
-            live["masked_shift", c] = masked_shift
-
-        def flip(c):
+        def flip(c, first):
             x_words = live["x", c][:].bitcast(F32)
-            for half in range(2):
-                flipped = psum_t.tile([P, 2, 2 * P], F32, name="flipped")
-                for jj in range(2):
-                    j = 2 * half + jj
-                    for u in range(2):
-                        nc.tensor.transpose(
-                            flipped[:, u, jj * P : (jj + 1) * P],
-                            x_words[:, j * WORDS + u : (j + 1) * WORDS : 2],
-                            ident[:],
-                        )
-                live["flipped", c, half] = flipped
+            flipped = psum_t.tile([P, 2, 2 * P], F32, name="flipped")
+            for j in range(first, min(first + 2, WIDTHS[c])):
+                for u in range(2):
+                    nc.tensor.transpose(
+                        flipped[:, u, (j - first) * P : (j - first + 1) * P],
+                        x_words[:, j * WORDS + u : (j + 1) * WORDS : 2],
+                        ident[:],
+                    )
+            live["flipped", c, first] = flipped
 
-        def group_x(c):
-            x_grouped = two.tile([P, CHUNK_COLS * PACK], BF16, align_bytes=64, name="x_grouped")
-            x_grouped_words = x_grouped[:].bitcast(F32).rearrange("q (n u) -> q n u", u=2)
-            for half in range(2):
-                nc.scalar.copy(
-                    out=x_grouped_words[:, half * 2 * P : (half + 1) * 2 * P, :],
-                    in_=live["flipped", c, half][:].rearrange("q u n -> q n u"),
-                )
-            live["x_grouped", c] = x_grouped
+        def group_x(c, first):
+            if first == 0:
+                live["x_grouped", c] = two.tile([P, WIDTHS[c] * E], BF16, align_bytes=64, name="x_grouped")
+            x_grouped_words = live["x_grouped", c][:].bitcast(F32).rearrange("q (n u) -> q n u", u=2)
+            n = min(2, WIDTHS[c] - first) * P
+            nc.scalar.copy(
+                out=x_grouped_words[:, first * P : first * P + n, :],
+                in_=live["flipped", c, first][:, :, 0:n].rearrange("q u n -> q n u"),
+            )
 
         def quantise_x(c):
-            x_codes = four.tile([P, CHUNK_COLS], U32, align_bytes=64, name="x_codes")
-            x_scales = four.tile([P, CHUNK_COLS], U8, align_bytes=64, name="x_scales")
+            cols = WIDTHS[c] * P
+            x_codes = four.tile([P, cols], U32, align_bytes=64, name="x_codes")
+            x_scales = four.tile([P, cols], U8, align_bytes=64, name="x_scales")
             nc.vector.quantize_mx(
                 out=x_codes[:].bitcast(FP8X4), scales=x_scales[:], in_=live["x_grouped", c][:]
             )
@@ -100,7 +92,7 @@ def tile_edgefeaturenet_pb_t_kernel(tc, h1, edge_mask, W2, b2, W3, b3, ln_g, ln_
             live["x_scales", c] = x_scales
 
         def layer1_pass(c, m):
-            acc1 = psum_1.tile([P, CHUNK_COLS], F32, name="acc1")
+            acc1 = psum_1.tile([P, WIDTHS[c] * P], F32, name="acc1")
             nc.tensor.matmul_mx(
                 out=acc1[:],
                 lhsT=w2_codes[:, m * P : (m + 1) * P].bitcast(FP8X4),
@@ -112,8 +104,9 @@ def tile_edgefeaturenet_pb_t_kernel(tc, h1, edge_mask, W2, b2, W3, b3, ln_g, ln_
             )
             live["acc1", c, m] = acc1
 
-        def relu_and_group_h(c):
-            h_planes = two.tile([P, PACK, CHUNK_COLS], BF16, name="h_planes")
+        def relu_h(c):
+            cols = WIDTHS[c] * P
+            h_planes = two.tile([P, PACK, cols], BF16, name="h_planes")
             for m in range(PACK):
                 nc.scalar.activation(
                     out=h_planes[:, m, :],
@@ -122,7 +115,11 @@ def tile_edgefeaturenet_pb_t_kernel(tc, h1, edge_mask, W2, b2, W3, b3, ln_g, ln_
                     bias=b2_f32[:, m : m + 1],
                     scale=1.0,
                 )
-            h_grouped = two.tile([P, CHUNK_COLS, PACK], BF16, align_bytes=64, name="h_grouped")
+            live["h_planes", c] = h_planes
+
+        def group_h(c):
+            h_planes = live["h_planes", c]
+            h_grouped = three.tile([P, WIDTHS[c] * P, PACK], BF16, align_bytes=64, name="h_grouped")
             nc.scalar.copy(
                 out=h_grouped[:].rearrange("p (n i) t -> p n t i", i=4),
                 in_=h_planes[:].rearrange("p t (n i) -> p n t i", i=4),
@@ -130,8 +127,9 @@ def tile_edgefeaturenet_pb_t_kernel(tc, h1, edge_mask, W2, b2, W3, b3, ln_g, ln_
             live["h_grouped", c] = h_grouped
 
         def quantise_h(c):
-            h_codes = three.tile([P, CHUNK_COLS], U32, align_bytes=64, name="h_codes")
-            h_scales = three.tile([P, CHUNK_COLS], U8, align_bytes=64, name="h_scales")
+            cols = WIDTHS[c] * P
+            h_codes = three.tile([P, cols], U32, align_bytes=64, name="h_codes")
+            h_scales = three.tile([P, cols], U8, align_bytes=64, name="h_scales")
             nc.vector.quantize_mx(
                 out=h_codes[:].bitcast(FP8X4),
                 scales=h_scales[:],
@@ -153,29 +151,71 @@ def tile_edgefeaturenet_pb_t_kernel(tc, h1, edge_mask, W2, b2, W3, b3, ln_g, ln_
             )
             live["acc2", c, j] = acc2
 
-        def add_bias_and_mean(c):
-            y = two.tile([P, TILES_PER_CHUNK, E], F32, name="y")
-            row_sum = three.tile([P, TILES_PER_CHUNK], F32, name="row_sum")
-            for j in range(TILES_PER_CHUNK):
-                nc.vector.scalar_tensor_tensor(
-                    out=y[:, j, :],
-                    in0=live["acc2", c, j][:],
-                    scalar=1.0,
-                    in1=b3_all[:],
-                    op0=ALU.mult,
-                    op1=ALU.add,
-                    accum_out=row_sum[:, j : j + 1],
+        def mask_diagonals(c):
+            diagonals = four.tile([P, PACK, P], BF16, name="diagonals")
+            for j in range(WIDTHS[c]):
+                if not shift_is_gpsimds(c, j):
+                    nc.gpsimd.tensor_scalar(
+                        out=diagonals[:, j, :],
+                        in0=ident_bf[:],
+                        scalar1=mask_f32[:, FIRST[c] + j : FIRST[c] + j + 1],
+                        scalar2=0.0,
+                        op0=ALU.mult,
+                        op1=ALU.add,
+                    )
+            live["diagonals", c] = diagonals
+
+        def shift_pass(c, j):
+            if not shift_is_gpsimds(c, j):
+                masked_shift = psum_s.tile([P, E], F32, name="masked_shift")
+                nc.tensor.matmul(
+                    out=masked_shift[:],
+                    lhsT=live["diagonals", c][:, j, :],
+                    rhs=shift_all[:],
+                    start=True,
+                    stop=True,
                 )
-            neg_mean = three.tile([P, TILES_PER_CHUNK], F32, name="neg_mean")
-            nc.vector.tensor_scalar(
-                out=neg_mean[:], in0=row_sum[:], scalar1=-1.0 / E, scalar2=None, op0=ALU.mult
+                live["masked_shift", c, j] = masked_shift
+
+        def shift_on_gpsimd(c):
+            for j in range(WIDTHS[c]):
+                if shift_is_gpsimds(c, j):
+                    gpsimds_shift = six.tile([P, E], F32, name="gpsimds_shift")
+                    nc.gpsimd.tensor_scalar(
+                        out=gpsimds_shift[:],
+                        in0=shift_all[:],
+                        scalar1=mask_f32[:, FIRST[c] + j : FIRST[c] + j + 1],
+                        scalar2=0.0,
+                        op0=ALU.mult,
+                        op1=ALU.add,
+                    )
+                    live["masked_shift", c, j] = gpsimds_shift
+
+        def open_sums(c):
+            live["y", c] = three.tile([P, WIDTHS[c], E], F32, name="y")
+            live["row_sum", c] = three.tile([P, WIDTHS[c]], F32, name="row_sum")
+
+        def add_bias(c, j):
+            nc.vector.scalar_tensor_tensor(
+                out=live["y", c][:, j, :],
+                in0=live["acc2", c, j][:],
+                scalar=1.0,
+                in1=b3_all[:],
+                op0=ALU.mult,
+                op1=ALU.add,
+                accum_out=live["row_sum", c][:, j : j + 1],
             )
-            live["y", c] = y
+
+        def negate_mean(c):
+            neg_mean = three.tile([P, WIDTHS[c]], F32, name="neg_mean")
+            nc.vector.tensor_scalar(
+                out=neg_mean[:], in0=live["row_sum", c][:], scalar1=-1.0 / E, scalar2=None, op0=ALU.mult
+            )
             live["neg_mean", c] = neg_mean
 
         def deviation(c):
-            square_sum = three.tile([P, TILES_PER_CHUNK], F32, name="square_sum")
-            for j in range(TILES_PER_CHUNK):
+            square_sum = three.tile([P, WIDTHS[c]], F32, name="square_sum")
+            for j in range(WIDTHS[c]):
                 squares = two.tile([P, E], F32, name="squares")
                 nc.scalar.activation(
                     out=squares[:],
@@ -185,52 +225,90 @@ def tile_edgefeaturenet_pb_t_kernel(tc, h1, edge_mask, W2, b2, W3, b3, ln_g, ln_
                     scale=1.0,
                     accum_out=square_sum[:, j : j + 1],
                 )
-            std = three.tile([P, TILES_PER_CHUNK], F32, name="std")
+            std = three.tile([P, WIDTHS[c]], F32, name="std")
             nc.scalar.activation(out=std[:], in_=square_sum[:], func=ACT.Sqrt, bias=eps[:, 0:1], scale=1.0 / E)
             live["std", c] = std
 
-        def centre_and_gain(c):
-            gained = three.tile([P, TILES_PER_CHUNK, E], F32, name="gained")
-            for j in range(TILES_PER_CHUNK):
-                nc.vector.scalar_tensor_tensor(
-                    out=gained[:, j, :],
-                    in0=live["y", c][:, j, :],
-                    scalar=live["neg_mean", c][:, j : j + 1],
-                    in1=gain_all[:],
-                    op0=ALU.add,
-                    op1=ALU.mult,
-                )
-            live["gained", c] = gained
-
-        def scale_shift_store(c):
-            inv_std = three.tile([P, TILES_PER_CHUNK], F32, name="inv_std")
-            nc.vector.reciprocal(out=inv_std[:], in_=live["std", c][:])
-            row_scale = three.tile([P, TILES_PER_CHUNK], F32, name="row_scale")
-            nc.vector.tensor_mul(
-                out=row_scale[:],
-                in0=inv_std[:],
-                in1=mask_f32[:, c * TILES_PER_CHUNK : (c + 1) * TILES_PER_CHUNK],
+        def centre_and_gain(c, j):
+            gained = four.tile([P, E], F32, name="gained") if j % 2 == 0 else four.tile([P, E], F32, name="gained_odd")
+            nc.vector.scalar_tensor_tensor(
+                out=gained[:],
+                in0=live["y", c][:, j, :],
+                scalar=live["neg_mean", c][:, j : j + 1],
+                in1=gain_psum[:],
+                op0=ALU.add,
+                op1=ALU.mult,
             )
-            result = three.tile([P, TILES_PER_CHUNK, E], F32, name="result")
-            for j in range(TILES_PER_CHUNK):
-                nc.vector.scalar_tensor_tensor(
-                    out=result[:, j, :],
-                    in0=live["gained", c][:, j, :],
-                    scalar=row_scale[:, j : j + 1],
-                    in1=live["masked_shift", c][:, j, :],
-                    op0=ALU.mult,
-                    op1=ALU.add,
+            live["gained", c, j] = gained
+
+        def centre_and_gain_on_gpsimd(c, j):
+            centred = two.tile([P, E], F32, name="centred")
+            nc.gpsimd.tensor_scalar(
+                out=centred[:],
+                in0=live["y", c][:, j, :],
+                scalar1=live["neg_mean", c][:, j : j + 1],
+                scalar2=1.0,
+                op0=ALU.add,
+                op1=ALU.mult,
+            )
+            gained = three.tile([P, E], F32, name="gpsimds_gained") if j % 2 == 0 else three.tile([P, E], F32, name="gpsimds_gained_odd")
+            nc.gpsimd.tensor_tensor(out=gained[:], in0=centred[:], in1=gain_all[:], op=ALU.mult)
+            live["gained", c, j] = gained
+
+        def gain_on_vector(c):
+            for j in range(WIDTHS[c]):
+                if not gain_is_gpsimds(c, j):
+                    centre_and_gain(c, j)
+
+        def gain_on_gpsimd(c):
+            for j in range(WIDTHS[c]):
+                if gain_is_gpsimds(c, j):
+                    centre_and_gain_on_gpsimd(c, j)
+
+        def invert_std(c):
+            inv_std = three.tile([P, WIDTHS[c]], F32, name="inv_std")
+            nc.vector.reciprocal(out=inv_std[:], in_=live["std", c][:])
+            live["inv_std", c] = inv_std
+
+        def mask_the_scale(c):
+            row_scale = three.tile([P, WIDTHS[c]], F32, name="row_scale")
+            nc.gpsimd.tensor_tensor(
+                out=row_scale[:],
+                in0=live["inv_std", c][:],
+                in1=mask_f32[:, FIRST[c] : FIRST[c] + WIDTHS[c]],
+                op=ALU.mult,
+            )
+            live["row_scale", c] = row_scale
+            live["result", c] = three.tile([P, WIDTHS[c], E], F32, name="result")
+
+        def scale_shift_store(c, j):
+            result = live["result", c]
+            nc.vector.scalar_tensor_tensor(
+                out=result[:, j, :],
+                in0=live["gained", c, j][:],
+                scalar=live["row_scale", c][:, j : j + 1],
+                in1=live["masked_shift", c, j][:],
+                op0=ALU.mult,
+                op1=ALU.add,
+            )
+            if j % 2 == 1 or j == WIDTHS[c] - 1:
+                first = j - j % 2
+                nc.sync.dma_start(
+                    out=out_rows[:, (FIRST[c] + first) * E : (FIRST[c] + j + 1) * E],
+                    in_=result[:, first : j + 1, :].rearrange("p j f -> p (j f)"),
                 )
-                if j % 2 == 1:
-                    first = (c * TILES_PER_CHUNK + j - 1) * E
-                    nc.sync.dma_start(
-                        out=out_rows[:, first : first + 2 * E],
-                        in_=result[:, j - 1 : j + 1, :].rearrange("p j f -> p (j f)"),
-                    )
 
         def when_in_range(step, c):
             if 0 <= c < N_CHUNKS:
                 step(c)
+
+        def for_tile(step, c, j):
+            if 0 <= c < N_CHUNKS and j < WIDTHS[c]:
+                step(c, j)
+
+        def for_plane(step, c, m):
+            if 0 <= c < N_CHUNKS:
+                step(c, m)
 
         load(0)
         load(1)
@@ -242,20 +320,22 @@ def tile_edgefeaturenet_pb_t_kernel(tc, h1, edge_mask, W2, b2, W3, b3, ln_g, ln_
         nc.scalar.dma_start(out=b2_bf[:], in_=b2.rearrange("(r m) -> r m", m=PACK))
         mask_bf = keep.tile([P, ROWS_PER_PARTITION], BF16)
         nc.scalar.dma_start(out=mask_bf[:], in_=mask_rows)
-        shift_all = keep.tile([P, E], BF16)
-        nc.scalar.dma_start(out=shift_all[:], in_=ln_b.partition_broadcast(P))
         b3_all = keep.tile([P, E], BF16)
         nc.scalar.dma_start(out=b3_all[:], in_=b3.partition_broadcast(P))
+        gain_all = keep.tile([P, E], BF16)
+        nc.scalar.dma_start(out=gain_all[:], in_=ln_g.partition_broadcast(P))
+        shift_all = keep.tile([P, E], BF16)
+        nc.scalar.dma_start(out=shift_all[:], in_=ln_b.partition_broadcast(P))
+
         ones = keep.tile([P, P], BF16)
         nc.vector.memset(ones[:], 1.0)
         gain_row = keep.tile([P, E], BF16)
         nc.vector.memset(gain_row[:], 0.0)
         nc.scalar.dma_start(out=gain_row[0:1, :], in_=ln_g.rearrange("(o f) -> o f", o=1))
-        gain_all = psum_keep.tile([P, E], F32)
-        nc.tensor.matmul(out=gain_all[:], lhsT=ones[:], rhs=gain_row[:], start=True, stop=True)
-
         ident = keep.tile([P, P], F32)
         make_identity(nc, ident[:])
+        ident_bf = keep.tile([P, P], BF16)
+        make_identity(nc, ident_bf[:])
         eps = keep.tile([P, 1], F32)
         nc.vector.memset(eps[:], EPS)
         table_warmer = keep.tile([P, 1], F32)
@@ -287,20 +367,43 @@ def tile_edgefeaturenet_pb_t_kernel(tc, h1, edge_mask, W2, b2, W3, b3, ln_g, ln_
         mask_f32 = keep.tile([P, ROWS_PER_PARTITION], F32)
         nc.vector.tensor_copy(out=mask_f32[:], in_=mask_bf[:])
 
-        for i in range(-3, N_CHUNKS + 1):
-            when_in_range(add_bias_and_mean, i)
-            when_in_range(scale_shift_store, i - 1)
-            when_in_range(relu_and_group_h, i + 1)
+        gain_psum = psum_keep.tile([P, E], F32)
+        for i in range(-7, N_CHUNKS):
             when_in_range(quantise_h, i + 1)
-            when_in_range(flip, i + 3)
-            when_in_range(group_x, i + 3)
+            when_in_range(quantise_x, i + 4)
+            when_in_range(negate_mean, i)
+            for_tile(group_x, i + 5, 0)
             when_in_range(deviation, i)
-            when_in_range(centre_and_gain, i)
-            when_in_range(quantise_x, i + 3)
+            for q in range(2):
+                for_tile(layer2_pass, i + 1, q)
             for q in range(PACK):
-                if 0 <= i + 1 < N_CHUNKS:
-                    layer2_pass(i + 1, q)
-                if 0 <= i + 2 < N_CHUNKS:
-                    layer1_pass(i + 2, q)
-            when_in_range(mask_the_shift, i + 2)
-            when_in_range(load, i + 5)
+                for_tile(shift_pass, i, q)
+            for q in range(2):
+                for_plane(layer1_pass, i + 3, q)
+            if i == GAIN_ROUND:
+                nc.tensor.matmul(out=gain_psum[:], lhsT=ones[:], rhs=gain_row[:], start=True, stop=True)
+            when_in_range(gain_on_gpsimd, i)
+            when_in_range(gain_on_vector, i)
+            when_in_range(open_sums, i + 1)
+            for_tile(add_bias, i + 1, 0)
+            for_tile(layer2_pass, i + 1, 2)
+            for_tile(add_bias, i + 1, 1)
+            for_tile(layer2_pass, i + 1, 3)
+            for_tile(add_bias, i + 1, 2)
+            when_in_range(invert_std, i)
+            for_tile(add_bias, i + 1, 3)
+            when_in_range(mask_the_scale, i)
+            when_in_range(mask_diagonals, i + 1)
+            when_in_range(shift_on_gpsimd, i + 1)
+            for_plane(layer1_pass, i + 3, 2)
+            for_tile(scale_shift_store, i, 0)
+            for_plane(layer1_pass, i + 3, 3)
+            for_tile(scale_shift_store, i, 1)
+            for_tile(scale_shift_store, i, 2)
+            for_tile(scale_shift_store, i, 3)
+            when_in_range(relu_h, i + 3)
+            for_tile(flip, i + 5, 2)
+            for_tile(group_x, i + 5, 2)
+            when_in_range(group_h, i + 3)
+            for_tile(flip, i + 6, 0)
+            when_in_range(load, i + 8)

@@ -18,9 +18,7 @@ ROWS = 2 * 64 * 64
 ROWS_PER_PARTITION = ROWS // P
 WORDS = E // 2
 EPS = 1e-5
-GAIN_ROUND = -2
-GPSIMD_TILES = 2
-WIDTHS = [1, 1, 2] + [4] * 14 + [2, 1, 1]
+WIDTHS = [4] * 16
 N_CHUNKS = len(WIDTHS)
 FIRST = [sum(WIDTHS[:c]) for c in range(N_CHUNKS)]
 
@@ -38,21 +36,17 @@ def tile_edgefeaturenet_pb_t_kernel(tc, h1, edge_mask, W2, b2, W3, b3, ln_g, ln_
         two = ctx.enter_context(tc.tile_pool(name="two", bufs=2))
         three = ctx.enter_context(tc.tile_pool(name="three", bufs=3))
         four = ctx.enter_context(tc.tile_pool(name="four", bufs=4))
-        six = ctx.enter_context(tc.tile_pool(name="six", bufs=6))
-        psum_t = ctx.enter_context(tc.psum_pool(name="psum_t", bufs=1))
+        eight = ctx.enter_context(tc.tile_pool(name="eight", bufs=8))
+        psum_t = ctx.enter_context(tc.psum_pool(name="psum_t", bufs=2))
         psum_1 = ctx.enter_context(tc.psum_pool(name="psum_1", bufs=2))
         psum_2 = ctx.enter_context(tc.psum_pool(name="psum_2", bufs=2))
         psum_s = ctx.enter_context(tc.psum_pool(name="psum_s", bufs=2))
-        psum_keep = ctx.enter_context(tc.psum_pool(name="psum_keep", bufs=1))
         ctx.enter_context(tc.manual_schedule())
 
         live = {}
 
         def shift_is_gpsimds(c, j):
-            return gain_is_gpsimds(c, j)
-
-        def gain_is_gpsimds(c, j):
-            return WIDTHS[c] == PACK and j >= PACK - GPSIMD_TILES
+            return j == PACK - 1
 
         def load(c):
             x = three.tile([P, WIDTHS[c] * E], BF16, name="x")
@@ -180,7 +174,7 @@ def tile_edgefeaturenet_pb_t_kernel(tc, h1, edge_mask, W2, b2, W3, b3, ln_g, ln_
         def shift_on_gpsimd(c):
             for j in range(WIDTHS[c]):
                 if shift_is_gpsimds(c, j):
-                    gpsimds_shift = six.tile([P, E], F32, name="gpsimds_shift")
+                    gpsimds_shift = three.tile([P, E], F32, name="gpsimds_shift")
                     nc.gpsimd.tensor_scalar(
                         out=gpsimds_shift[:],
                         in0=shift_all[:],
@@ -230,40 +224,20 @@ def tile_edgefeaturenet_pb_t_kernel(tc, h1, edge_mask, W2, b2, W3, b3, ln_g, ln_
             live["std", c] = std
 
         def centre_and_gain(c, j):
-            gained = four.tile([P, E], F32, name="gained") if j % 2 == 0 else four.tile([P, E], F32, name="gained_odd")
+            gained = eight.tile([P, E], F32, name="gained")
             nc.vector.scalar_tensor_tensor(
                 out=gained[:],
                 in0=live["y", c][:, j, :],
                 scalar=live["neg_mean", c][:, j : j + 1],
-                in1=gain_psum[:],
+                in1=gain_all[:],
                 op0=ALU.add,
                 op1=ALU.mult,
             )
-            live["gained", c, j] = gained
-
-        def centre_and_gain_on_gpsimd(c, j):
-            centred = two.tile([P, E], F32, name="centred")
-            nc.gpsimd.tensor_scalar(
-                out=centred[:],
-                in0=live["y", c][:, j, :],
-                scalar1=live["neg_mean", c][:, j : j + 1],
-                scalar2=1.0,
-                op0=ALU.add,
-                op1=ALU.mult,
-            )
-            gained = three.tile([P, E], F32, name="gpsimds_gained") if j % 2 == 0 else three.tile([P, E], F32, name="gpsimds_gained_odd")
-            nc.gpsimd.tensor_tensor(out=gained[:], in0=centred[:], in1=gain_all[:], op=ALU.mult)
             live["gained", c, j] = gained
 
         def gain_on_vector(c):
             for j in range(WIDTHS[c]):
-                if not gain_is_gpsimds(c, j):
-                    centre_and_gain(c, j)
-
-        def gain_on_gpsimd(c):
-            for j in range(WIDTHS[c]):
-                if gain_is_gpsimds(c, j):
-                    centre_and_gain_on_gpsimd(c, j)
+                centre_and_gain(c, j)
 
         def invert_std(c):
             inv_std = three.tile([P, WIDTHS[c]], F32, name="inv_std")
@@ -327,11 +301,6 @@ def tile_edgefeaturenet_pb_t_kernel(tc, h1, edge_mask, W2, b2, W3, b3, ln_g, ln_
         shift_all = keep.tile([P, E], BF16)
         nc.scalar.dma_start(out=shift_all[:], in_=ln_b.partition_broadcast(P))
 
-        ones = keep.tile([P, P], BF16)
-        nc.vector.memset(ones[:], 1.0)
-        gain_row = keep.tile([P, E], BF16)
-        nc.vector.memset(gain_row[:], 0.0)
-        nc.scalar.dma_start(out=gain_row[0:1, :], in_=ln_g.rearrange("(o f) -> o f", o=1))
         ident = keep.tile([P, P], F32)
         make_identity(nc, ident[:])
         ident_bf = keep.tile([P, P], BF16)
@@ -367,43 +336,40 @@ def tile_edgefeaturenet_pb_t_kernel(tc, h1, edge_mask, W2, b2, W3, b3, ln_g, ln_
         mask_f32 = keep.tile([P, ROWS_PER_PARTITION], F32)
         nc.vector.tensor_copy(out=mask_f32[:], in_=mask_bf[:])
 
-        gain_psum = psum_keep.tile([P, E], F32)
-        for i in range(-7, N_CHUNKS):
+        for i in range(-5, N_CHUNKS):
             when_in_range(quantise_h, i + 1)
-            when_in_range(quantise_x, i + 4)
+            when_in_range(quantise_x, i + 3)
             when_in_range(negate_mean, i)
-            for_tile(group_x, i + 5, 0)
+            for_tile(group_x, i + 4, 0)
+            for_tile(group_x, i + 4, 2)
             when_in_range(deviation, i)
             for q in range(2):
                 for_tile(layer2_pass, i + 1, q)
-            for q in range(PACK):
-                for_tile(shift_pass, i, q)
             for q in range(2):
-                for_plane(layer1_pass, i + 3, q)
-            if i == GAIN_ROUND:
-                nc.tensor.matmul(out=gain_psum[:], lhsT=ones[:], rhs=gain_row[:], start=True, stop=True)
-            when_in_range(gain_on_gpsimd, i)
+                for_plane(layer1_pass, i + 2, q)
+            for q in range(2):
+                for_tile(shift_pass, i, q)
             when_in_range(gain_on_vector, i)
             when_in_range(open_sums, i + 1)
             for_tile(add_bias, i + 1, 0)
             for_tile(layer2_pass, i + 1, 2)
+            for_plane(layer1_pass, i + 2, 2)
             for_tile(add_bias, i + 1, 1)
             for_tile(layer2_pass, i + 1, 3)
+            for_plane(layer1_pass, i + 2, 3)
             for_tile(add_bias, i + 1, 2)
             when_in_range(invert_std, i)
             for_tile(add_bias, i + 1, 3)
             when_in_range(mask_the_scale, i)
             when_in_range(mask_diagonals, i + 1)
             when_in_range(shift_on_gpsimd, i + 1)
-            for_plane(layer1_pass, i + 3, 2)
             for_tile(scale_shift_store, i, 0)
-            for_plane(layer1_pass, i + 3, 3)
+            for_tile(shift_pass, i, 2)
             for_tile(scale_shift_store, i, 1)
             for_tile(scale_shift_store, i, 2)
             for_tile(scale_shift_store, i, 3)
-            when_in_range(relu_h, i + 3)
+            when_in_range(relu_h, i + 2)
+            when_in_range(group_h, i + 2)
+            for_tile(flip, i + 5, 0)
             for_tile(flip, i + 5, 2)
-            for_tile(group_x, i + 5, 2)
-            when_in_range(group_h, i + 3)
-            for_tile(flip, i + 6, 0)
-            when_in_range(load, i + 8)
+            when_in_range(load, i + 7)

@@ -114,11 +114,17 @@ def tile_edgefeaturenet_pb_t_kernel(tc, h1, edge_mask, W2, b2, W3, b3, ln_g, ln_
         def group_h(c):
             h_planes = live["h_planes", c]
             h_grouped = three.tile([P, WIDTHS[c] * P, PACK], BF16, align_bytes=64, name="h_grouped")
-            nc.scalar.copy(
-                out=h_grouped[:].rearrange("p (n i) t -> p n t i", i=4),
-                in_=h_planes[:].rearrange("p t (n i) -> p n t i", i=4),
-            )
             live["h_grouped", c] = h_grouped
+            regroup(nc.scalar.copy, c, 0, WIDTHS[c] * P // 2)
+
+        def regroup(copy, c, first, last):
+            copy(
+                out=live["h_grouped", c][:, first:last, :].rearrange("p (n i) t -> p n t i", i=4),
+                in_=live["h_planes", c][:, :, first:last].rearrange("p t (n i) -> p n t i", i=4),
+            )
+
+        def regroup_on_vector(c):
+            regroup(nc.vector.tensor_copy, c, WIDTHS[c] * P // 2, WIDTHS[c] * P)
 
         def quantise_h(c):
             cols = WIDTHS[c] * P
@@ -367,9 +373,10 @@ def tile_edgefeaturenet_pb_t_kernel(tc, h1, edge_mask, W2, b2, W3, b3, ln_g, ln_
             for_tile(shift_pass, i, 2)
             for_tile(scale_shift_store, i, 1)
             for_tile(scale_shift_store, i, 2)
-            for_tile(scale_shift_store, i, 3)
             when_in_range(relu_h, i + 2)
             when_in_range(group_h, i + 2)
+            when_in_range(regroup_on_vector, i + 2)
+            for_tile(scale_shift_store, i, 3)
             for_tile(flip, i + 5, 0)
             for_tile(flip, i + 5, 2)
             when_in_range(load, i + 7)

@@ -18,6 +18,7 @@ ROWS = 2 * 64 * 64
 ROWS_PER_PARTITION = ROWS // P
 WORDS = E // 2
 EPS = 1e-5
+GPSIMD_TILES = 2
 WIDTHS = [4] * 16
 N_CHUNKS = len(WIDTHS)
 FIRST = [sum(WIDTHS[:c]) for c in range(N_CHUNKS)]
@@ -40,13 +41,13 @@ def tile_edgefeaturenet_pb_t_kernel(tc, h1, edge_mask, W2, b2, W3, b3, ln_g, ln_
         psum_t = ctx.enter_context(tc.psum_pool(name="psum_t", bufs=2))
         psum_1 = ctx.enter_context(tc.psum_pool(name="psum_1", bufs=2))
         psum_2 = ctx.enter_context(tc.psum_pool(name="psum_2", bufs=2))
-        psum_s = ctx.enter_context(tc.psum_pool(name="psum_s", bufs=2))
+        psum_keep = ctx.enter_context(tc.psum_pool(name="psum_keep", bufs=1))
         ctx.enter_context(tc.manual_schedule())
 
         live = {}
 
-        def shift_is_gpsimds(c, j):
-            return j == PACK - 1
+        def gain_is_gpsimds(c, j):
+            return WIDTHS[c] == PACK and j >= PACK - GPSIMD_TILES
 
         def load(c):
             x = three.tile([P, WIDTHS[c] * E], BF16, name="x")
@@ -151,46 +152,6 @@ def tile_edgefeaturenet_pb_t_kernel(tc, h1, edge_mask, W2, b2, W3, b3, ln_g, ln_
             )
             live["acc2", c, j] = acc2
 
-        def mask_diagonals(c):
-            diagonals = four.tile([P, PACK, P], BF16, name="diagonals")
-            for j in range(WIDTHS[c]):
-                if not shift_is_gpsimds(c, j):
-                    nc.gpsimd.tensor_scalar(
-                        out=diagonals[:, j, :],
-                        in0=ident_bf[:],
-                        scalar1=mask_f32[:, FIRST[c] + j : FIRST[c] + j + 1],
-                        scalar2=0.0,
-                        op0=ALU.mult,
-                        op1=ALU.add,
-                    )
-            live["diagonals", c] = diagonals
-
-        def shift_pass(c, j):
-            if not shift_is_gpsimds(c, j):
-                masked_shift = psum_s.tile([P, E], F32, name="masked_shift")
-                nc.tensor.matmul(
-                    out=masked_shift[:],
-                    lhsT=live["diagonals", c][:, j, :],
-                    rhs=shift_all[:],
-                    start=True,
-                    stop=True,
-                )
-                live["masked_shift", c, j] = masked_shift
-
-        def shift_on_gpsimd(c):
-            for j in range(WIDTHS[c]):
-                if shift_is_gpsimds(c, j):
-                    gpsimds_shift = three.tile([P, E], F32, name="gpsimds_shift")
-                    nc.gpsimd.tensor_scalar(
-                        out=gpsimds_shift[:],
-                        in0=shift_all[:],
-                        scalar1=mask_f32[:, FIRST[c] + j : FIRST[c] + j + 1],
-                        scalar2=0.0,
-                        op0=ALU.mult,
-                        op1=ALU.add,
-                    )
-                    live["masked_shift", c, j] = gpsimds_shift
-
         def open_sums(c):
             live["y", c] = three.tile([P, WIDTHS[c], E], F32, name="y")
             live["row_sum", c] = three.tile([P, WIDTHS[c]], F32, name="row_sum")
@@ -208,9 +169,7 @@ def tile_edgefeaturenet_pb_t_kernel(tc, h1, edge_mask, W2, b2, W3, b3, ln_g, ln_
 
         def negate_mean(c):
             neg_mean = three.tile([P, WIDTHS[c]], F32, name="neg_mean")
-            nc.vector.tensor_scalar(
-                out=neg_mean[:], in0=live["row_sum", c][:], scalar1=-1.0 / E, scalar2=None, op0=ALU.mult
-            )
+            nc.scalar.activation(out=neg_mean[:], in_=live["row_sum", c][:], func=ACT.Copy, scale=-1.0 / E)
             live["neg_mean", c] = neg_mean
 
         def deviation(c):
@@ -229,28 +188,12 @@ def tile_edgefeaturenet_pb_t_kernel(tc, h1, edge_mask, W2, b2, W3, b3, ln_g, ln_
             nc.scalar.activation(out=std[:], in_=square_sum[:], func=ACT.Sqrt, bias=eps[:, 0:1], scale=1.0 / E)
             live["std", c] = std
 
-        def centre_and_gain(c, j):
-            gained = eight.tile([P, E], F32, name="gained")
-            nc.vector.scalar_tensor_tensor(
-                out=gained[:],
-                in0=live["y", c][:, j, :],
-                scalar=live["neg_mean", c][:, j : j + 1],
-                in1=gain_all[:],
-                op0=ALU.add,
-                op1=ALU.mult,
-            )
-            live["gained", c, j] = gained
-
-        def gain_on_vector(c):
-            for j in range(WIDTHS[c]):
-                centre_and_gain(c, j)
-
         def invert_std(c):
             inv_std = three.tile([P, WIDTHS[c]], F32, name="inv_std")
             nc.vector.reciprocal(out=inv_std[:], in_=live["std", c][:])
             live["inv_std", c] = inv_std
 
-        def mask_the_scale(c):
+        def row_factors(c):
             row_scale = three.tile([P, WIDTHS[c]], F32, name="row_scale")
             nc.gpsimd.tensor_tensor(
                 out=row_scale[:],
@@ -258,16 +201,44 @@ def tile_edgefeaturenet_pb_t_kernel(tc, h1, edge_mask, W2, b2, W3, b3, ln_g, ln_
                 in1=mask_f32[:, FIRST[c] : FIRST[c] + WIDTHS[c]],
                 op=ALU.mult,
             )
+            row_offset = three.tile([P, WIDTHS[c]], F32, name="row_offset")
+            nc.gpsimd.tensor_tensor(out=row_offset[:], in0=live["neg_mean", c][:], in1=row_scale[:], op=ALU.mult)
             live["row_scale", c] = row_scale
-            live["result", c] = three.tile([P, WIDTHS[c], E], F32, name="result")
+            live["row_offset", c] = row_offset
 
-        def scale_shift_store(c, j):
+        def standardise(c):
+            for j in range(WIDTHS[c]):
+                standard = eight.tile([P, E], F32, name="standard")
+                nc.gpsimd.tensor_scalar(
+                    out=standard[:],
+                    in0=live["y", c][:, j, :],
+                    scalar1=live["row_scale", c][:, j : j + 1],
+                    scalar2=live["row_offset", c][:, j : j + 1],
+                    op0=ALU.mult,
+                    op1=ALU.add,
+                )
+                live["standard", c, j] = standard
+                if gain_is_gpsimds(c, j):
+                    gained = four.tile([P, E], F32, name="gpsimds_gained")
+                    nc.gpsimd.tensor_tensor(out=gained[:], in0=standard[:], in1=gain_all[:], op=ALU.mult)
+                    live["gained", c, j] = gained
+
+        def gain_on_vector(c, j):
+            if not gain_is_gpsimds(c, j):
+                gained = four.tile([P, E], F32, name="gained")
+                nc.vector.tensor_tensor(out=gained[:], in0=live["standard", c, j][:], in1=gain_psum[:], op=ALU.mult)
+                live["gained", c, j] = gained
+
+        def shift_and_store(c, j):
+            if j == 0:
+                live["result", c] = three.tile([P, WIDTHS[c], E], F32, name="result")
             result = live["result", c]
+            t = FIRST[c] + j
             nc.vector.scalar_tensor_tensor(
                 out=result[:, j, :],
-                in0=live["gained", c, j][:],
-                scalar=live["row_scale", c][:, j : j + 1],
-                in1=live["masked_shift", c, j][:],
+                in0=shift_psum[:],
+                scalar=mask_f32[:, t : t + 1],
+                in1=live["gained", c, j][:],
                 op0=ALU.mult,
                 op1=ALU.add,
             )
@@ -304,13 +275,15 @@ def tile_edgefeaturenet_pb_t_kernel(tc, h1, edge_mask, W2, b2, W3, b3, ln_g, ln_
         nc.scalar.dma_start(out=b3_all[:], in_=b3.partition_broadcast(P))
         gain_all = keep.tile([P, E], BF16)
         nc.scalar.dma_start(out=gain_all[:], in_=ln_g.partition_broadcast(P))
-        shift_all = keep.tile([P, E], BF16)
-        nc.scalar.dma_start(out=shift_all[:], in_=ln_b.partition_broadcast(P))
+        ones = keep.tile([P, P], BF16)
+        nc.vector.memset(ones[:], 1.0)
+        vector_rows = keep.tile([P, 2, E], BF16)
+        nc.vector.memset(vector_rows[:], 0.0)
+        nc.scalar.dma_start(out=vector_rows[0:1, 0, :], in_=ln_g.rearrange("(o f) -> o f", o=1))
+        nc.scalar.dma_start(out=vector_rows[0:1, 1, :], in_=ln_b.rearrange("(o f) -> o f", o=1))
 
         ident = keep.tile([P, P], F32)
         make_identity(nc, ident[:])
-        ident_bf = keep.tile([P, P], BF16)
-        make_identity(nc, ident_bf[:])
         eps = keep.tile([P, 1], F32)
         nc.vector.memset(eps[:], EPS)
         table_warmer = keep.tile([P, 1], F32)
@@ -342,41 +315,43 @@ def tile_edgefeaturenet_pb_t_kernel(tc, h1, edge_mask, W2, b2, W3, b3, ln_g, ln_
         mask_f32 = keep.tile([P, ROWS_PER_PARTITION], F32)
         nc.vector.tensor_copy(out=mask_f32[:], in_=mask_bf[:])
 
-        for i in range(-5, N_CHUNKS):
-            when_in_range(quantise_h, i + 1)
-            when_in_range(quantise_x, i + 3)
-            when_in_range(negate_mean, i)
-            for_tile(group_x, i + 4, 0)
-            for_tile(group_x, i + 4, 2)
-            when_in_range(deviation, i)
-            for q in range(2):
-                for_tile(layer2_pass, i + 1, q)
+        gain_psum = psum_keep.tile([P, E], F32)
+        shift_psum = psum_keep.tile([P, E], F32)
+        for i in range(-5, N_CHUNKS + 1):
+            if i == -2:
+                nc.tensor.matmul(out=gain_psum[:], lhsT=ones[:], rhs=vector_rows[:, 0, :], start=True, stop=True)
+                nc.tensor.matmul(out=shift_psum[:], lhsT=ones[:], rhs=vector_rows[:, 1, :], start=True, stop=True)
             for q in range(2):
                 for_plane(layer1_pass, i + 2, q)
+            when_in_range(negate_mean, i)
+            when_in_range(deviation, i)
+            when_in_range(regroup_on_vector, i + 1)
+            when_in_range(quantise_x, i + 3)
+            when_in_range(quantise_h, i + 1)
+            for_tile(shift_and_store, i - 1, 2)
+            for_tile(shift_and_store, i - 1, 3)
+            when_in_range(invert_std, i)
+            when_in_range(row_factors, i)
+            when_in_range(standardise, i)
             for q in range(2):
-                for_tile(shift_pass, i, q)
-            when_in_range(gain_on_vector, i)
+                for_tile(layer2_pass, i + 1, q)
             when_in_range(open_sums, i + 1)
             for_tile(add_bias, i + 1, 0)
-            for_tile(layer2_pass, i + 1, 2)
             for_plane(layer1_pass, i + 2, 2)
+            for_tile(layer2_pass, i + 1, 2)
             for_tile(add_bias, i + 1, 1)
-            for_tile(layer2_pass, i + 1, 3)
             for_plane(layer1_pass, i + 2, 3)
+            for_tile(layer2_pass, i + 1, 3)
             for_tile(add_bias, i + 1, 2)
-            when_in_range(invert_std, i)
             for_tile(add_bias, i + 1, 3)
-            when_in_range(mask_the_scale, i)
-            when_in_range(mask_diagonals, i + 1)
-            when_in_range(shift_on_gpsimd, i + 1)
-            for_tile(scale_shift_store, i, 0)
-            for_tile(shift_pass, i, 2)
-            for_tile(scale_shift_store, i, 1)
-            for_tile(scale_shift_store, i, 2)
+            for_tile(gain_on_vector, i, 0)
+            for_tile(gain_on_vector, i, 1)
+            for_tile(shift_and_store, i, 0)
+            for_tile(shift_and_store, i, 1)
             when_in_range(relu_h, i + 2)
             when_in_range(group_h, i + 2)
-            when_in_range(regroup_on_vector, i + 2)
-            for_tile(scale_shift_store, i, 3)
-            for_tile(flip, i + 5, 0)
-            for_tile(flip, i + 5, 2)
-            when_in_range(load, i + 7)
+            for_tile(flip, i + 4, 0)
+            for_tile(flip, i + 4, 2)
+            for_tile(group_x, i + 4, 0)
+            for_tile(group_x, i + 4, 2)
+            when_in_range(load, i + 6)

@@ -18,7 +18,7 @@ ROWS = 2 * 64 * 64
 ROWS_PER_PARTITION = ROWS // P
 WORDS = E // 2
 EPS = 1e-5
-GPSIMD_TILES = 2
+VECTOR_COLUMNS = 256
 WIDTHS = [4] * 16
 N_CHUNKS = len(WIDTHS)
 FIRST = [sum(WIDTHS[:c]) for c in range(N_CHUNKS)]
@@ -42,15 +42,16 @@ def tile_edgefeaturenet_pb_t_kernel(tc, h1, edge_mask, W2, b2, W3, b3, ln_g, ln_
         psum_1 = ctx.enter_context(tc.psum_pool(name="psum_1", bufs=2))
         psum_2 = ctx.enter_context(tc.psum_pool(name="psum_2", bufs=2))
         psum_keep = ctx.enter_context(tc.psum_pool(name="psum_keep", bufs=1))
+        psum_s = ctx.enter_context(tc.psum_pool(name="psum_s", bufs=1))
         ctx.enter_context(tc.manual_schedule())
 
         live = {}
 
-        def gain_is_gpsimds(c, j):
-            return WIDTHS[c] == PACK and j >= PACK - GPSIMD_TILES
+        def tile_is_gpsimds(j):
+            return j >= 2
 
         def load(c):
-            x = three.tile([P, WIDTHS[c] * E], BF16, name="x")
+            x = four.tile([P, WIDTHS[c] * E], BF16, name="x")
             nc.sync.dma_start(out=x[:], in_=h1_rows[:, FIRST[c] * E : (FIRST[c] + WIDTHS[c]) * E])
             live["x", c] = x
 
@@ -99,24 +100,18 @@ def tile_edgefeaturenet_pb_t_kernel(tc, h1, edge_mask, W2, b2, W3, b3, ln_g, ln_
             )
             live["acc1", c, m] = acc1
 
-        def relu_h(c):
-            cols = WIDTHS[c] * P
-            h_planes = two.tile([P, PACK, cols], BF16, name="h_planes")
-            for m in range(PACK):
-                nc.scalar.activation(
-                    out=h_planes[:, m, :],
-                    in_=live["acc1", c, m][:],
-                    func=ACT.Relu,
-                    bias=b2_f32[:, m : m + 1],
-                    scale=1.0,
-                )
-            live["h_planes", c] = h_planes
+        def relu_h1(c, m):
+            if m == 0:
+                live["h_planes", c] = three.tile([P, PACK, WIDTHS[c] * P], BF16, name="h_planes")
+            plane = live["h_planes", c][:, m, :]
+            bias = b2_bf[:, m : m + 1]
+            nc.scalar.activation(out=plane, in_=live["acc1", c, m][:], func=ACT.Relu, bias=bias, scale=1.0)
 
         def group_h(c):
             h_planes = live["h_planes", c]
             h_grouped = three.tile([P, WIDTHS[c] * P, PACK], BF16, align_bytes=64, name="h_grouped")
             live["h_grouped", c] = h_grouped
-            regroup(nc.scalar.copy, c, 0, WIDTHS[c] * P // 2)
+            regroup(nc.scalar.copy, c, 0, WIDTHS[c] * P - VECTOR_COLUMNS)
 
         def regroup(copy, c, first, last):
             copy(
@@ -125,7 +120,7 @@ def tile_edgefeaturenet_pb_t_kernel(tc, h1, edge_mask, W2, b2, W3, b3, ln_g, ln_
             )
 
         def regroup_on_vector(c):
-            regroup(nc.vector.tensor_copy, c, WIDTHS[c] * P // 2, WIDTHS[c] * P)
+            regroup(nc.vector.tensor_copy, c, WIDTHS[c] * P - VECTOR_COLUMNS, WIDTHS[c] * P)
 
         def quantise_h(c):
             cols = WIDTHS[c] * P
@@ -206,52 +201,72 @@ def tile_edgefeaturenet_pb_t_kernel(tc, h1, edge_mask, W2, b2, W3, b3, ln_g, ln_
             live["row_scale", c] = row_scale
             live["row_offset", c] = row_offset
 
-        def standardise(c):
-            for j in range(WIDTHS[c]):
-                standard = eight.tile([P, E], F32, name="standard")
-                nc.gpsimd.tensor_scalar(
-                    out=standard[:],
-                    in0=live["y", c][:, j, :],
-                    scalar1=live["row_scale", c][:, j : j + 1],
-                    scalar2=live["row_offset", c][:, j : j + 1],
-                    op0=ALU.mult,
-                    op1=ALU.add,
-                )
-                live["standard", c, j] = standard
-                if gain_is_gpsimds(c, j):
-                    gained = four.tile([P, E], F32, name="gpsimds_gained")
-                    nc.gpsimd.tensor_tensor(out=gained[:], in0=standard[:], in1=gain_all[:], op=ALU.mult)
-                    live["gained", c, j] = gained
+        def gain_on_gpsimd(c, j):
+            standard = two.tile([P, E], F32, name="standard")
+            nc.gpsimd.tensor_scalar(
+                out=standard[:],
+                in0=live["y", c][:, j, :],
+                scalar1=live["row_scale", c][:, j : j + 1],
+                scalar2=live["row_offset", c][:, j : j + 1],
+                op0=ALU.mult,
+                op1=ALU.add,
+            )
+            gained = four.tile([P, E], F32, name="gpsimds_gained")
+            nc.gpsimd.tensor_tensor(out=gained[:], in0=standard[:], in1=gain_all[:], op=ALU.mult)
+            live["gained", c, j] = gained
 
         def gain_on_vector(c, j):
-            if not gain_is_gpsimds(c, j):
-                gained = four.tile([P, E], F32, name="gained")
-                nc.vector.tensor_tensor(out=gained[:], in0=live["standard", c, j][:], in1=gain_psum[:], op=ALU.mult)
-                live["gained", c, j] = gained
+            gained = four.tile([P, E], F32, name="gained")
+            nc.vector.scalar_tensor_tensor(
+                out=gained[:],
+                in0=live["y", c][:, j, :],
+                scalar=live["neg_mean", c][:, j : j + 1],
+                in1=gain_psum,
+                op0=ALU.add,
+                op1=ALU.mult,
+            )
+            live["gained", c, j] = gained
+
+        def shift_pass(c, j):
+            masked_shift = psum_s.tile([P, E], F32, name="masked_shift")
+            nc.tensor.matmul(
+                out=masked_shift[:], lhsT=diagonals[:, 2 * c + j, :], rhs=shift_all[:], start=True, stop=True
+            )
+            live["masked_shift", c, j] = masked_shift
 
         def shift_and_store(c, j):
             if j == 0:
                 live["result", c] = three.tile([P, WIDTHS[c], E], F32, name="result")
             result = live["result", c]
             t = FIRST[c] + j
-            nc.vector.scalar_tensor_tensor(
-                out=result[:, j, :],
-                in0=shift_psum[:],
-                scalar=mask_f32[:, t : t + 1],
-                in1=live["gained", c, j][:],
-                op0=ALU.mult,
-                op1=ALU.add,
-            )
-            if j % 2 == 1 or j == WIDTHS[c] - 1:
-                first = j - j % 2
+            if tile_is_gpsimds(j):
+                nc.vector.scalar_tensor_tensor(
+                    out=result[:, j, :],
+                    in0=shift_psum,
+                    scalar=mask_f32[:, t : t + 1],
+                    in1=live["gained", c, j][:],
+                    op0=ALU.mult,
+                    op1=ALU.add,
+                )
+            else:
+                nc.vector.scalar_tensor_tensor(
+                    out=result[:, j, :],
+                    in0=live["gained", c, j][:],
+                    scalar=live["row_scale", c][:, j : j + 1],
+                    in1=live["masked_shift", c, j][:],
+                    op0=ALU.mult,
+                    op1=ALU.add,
+                )
+            if j % 2 == 1:
+                first = j - 1
                 nc.sync.dma_start(
                     out=out_rows[:, (FIRST[c] + first) * E : (FIRST[c] + j + 1) * E],
                     in_=result[:, first : j + 1, :].rearrange("p j f -> p (j f)"),
                 )
 
-        def when_in_range(step, c):
+        def when_in_range(step, c, *rest):
             if 0 <= c < N_CHUNKS:
-                step(c)
+                step(c, *rest)
 
         def for_tile(step, c, j):
             if 0 <= c < N_CHUNKS and j < WIDTHS[c]:
@@ -261,12 +276,14 @@ def tile_edgefeaturenet_pb_t_kernel(tc, h1, edge_mask, W2, b2, W3, b3, ln_g, ln_
             if 0 <= c < N_CHUNKS:
                 step(c, m)
 
+        w2_raw = keep.tile([P, PACK, E], BF16)
+        nc.sync.dma_start(out=w2_raw[:], in_=W2.rearrange("(q t) n -> q t n", t=PACK))
         load(0)
         load(1)
-        w2_raw = keep.tile([P, PACK, E], BF16)
-        nc.scalar.dma_start(out=w2_raw[:], in_=W2.rearrange("(q t) n -> q t n", t=PACK))
         w3_raw = keep.tile([P, PACK, E], BF16)
-        nc.scalar.dma_start(out=w3_raw[:], in_=W3.rearrange("(p t) n -> p t n", t=PACK))
+        nc.sync.dma_start(out=w3_raw[:], in_=W3.rearrange("(p t) n -> p t n", t=PACK))
+        load(2)
+        load(3)
         b2_bf = keep.tile([P, PACK], BF16)
         nc.scalar.dma_start(out=b2_bf[:], in_=b2.rearrange("(r m) -> r m", m=PACK))
         mask_bf = keep.tile([P, ROWS_PER_PARTITION], BF16)
@@ -275,6 +292,8 @@ def tile_edgefeaturenet_pb_t_kernel(tc, h1, edge_mask, W2, b2, W3, b3, ln_g, ln_
         nc.scalar.dma_start(out=b3_all[:], in_=b3.partition_broadcast(P))
         gain_all = keep.tile([P, E], BF16)
         nc.scalar.dma_start(out=gain_all[:], in_=ln_g.partition_broadcast(P))
+        shift_all = keep.tile([P, E], BF16)
+        nc.scalar.dma_start(out=shift_all[:], in_=ln_b.partition_broadcast(P))
         ones = keep.tile([P, P], BF16)
         nc.vector.memset(ones[:], 1.0)
         vector_rows = keep.tile([P, 2, E], BF16)
@@ -284,6 +303,8 @@ def tile_edgefeaturenet_pb_t_kernel(tc, h1, edge_mask, W2, b2, W3, b3, ln_g, ln_
 
         ident = keep.tile([P, P], F32)
         make_identity(nc, ident[:])
+        ident_bf = keep.tile([P, P], BF16)
+        make_identity(nc, ident_bf[:])
         eps = keep.tile([P, 1], F32)
         nc.vector.memset(eps[:], EPS)
         table_warmer = keep.tile([P, 1], F32)
@@ -294,8 +315,6 @@ def tile_edgefeaturenet_pb_t_kernel(tc, h1, edge_mask, W2, b2, W3, b3, ln_g, ln_
             out=w2_grouped[:].rearrange("q (m r) t -> q m r t", m=PACK),
             in_=w2_raw[:].rearrange("q t (r m) -> q m r t", m=PACK),
         )
-        w3_grouped = keep.tile([P, E, PACK], BF16, align_bytes=64)
-        nc.vector.tensor_copy(out=w3_grouped[:], in_=w3_raw[:].rearrange("p t n -> p n t"))
         w2_codes = keep.tile([P, E], U32, align_bytes=64)
         w2_scales = keep.tile([P, E], U8, align_bytes=64)
         nc.vector.quantize_mx(
@@ -303,55 +322,85 @@ def tile_edgefeaturenet_pb_t_kernel(tc, h1, edge_mask, W2, b2, W3, b3, ln_g, ln_
             scales=w2_scales[:],
             in_=w2_grouped[:].rearrange("q n t -> q (n t)"),
         )
+        mask_f32 = keep.tile([P, ROWS_PER_PARTITION], F32)
+        nc.gpsimd.tensor_copy(out=mask_f32[:], in_=mask_bf[:])
+        diagonals = keep.tile([P, 2 * N_CHUNKS, P], BF16)
+        for c in range(N_CHUNKS):
+            for j in range(2):
+                nc.gpsimd.tensor_scalar(
+                    out=diagonals[:, 2 * c + j, :],
+                    in0=ident_bf[:],
+                    scalar1=mask_f32[:, FIRST[c] + j : FIRST[c] + j + 1],
+                    scalar2=0.0,
+                    op0=ALU.mult,
+                    op1=ALU.add,
+                )
+
+        w3_grouped = keep.tile([P, E, PACK], BF16, align_bytes=64)
         w3_codes = keep.tile([P, E], U32, align_bytes=64)
         w3_scales = keep.tile([P, E], U8, align_bytes=64)
-        nc.vector.quantize_mx(
-            out=w3_codes[:].bitcast(FP8X4),
-            scales=w3_scales[:],
-            in_=w3_grouped[:].rearrange("p n t -> p (n t)"),
-        )
-        b2_f32 = keep.tile([P, PACK], F32)
-        nc.vector.tensor_copy(out=b2_f32[:], in_=b2_bf[:])
-        mask_f32 = keep.tile([P, ROWS_PER_PARTITION], F32)
-        nc.vector.tensor_copy(out=mask_f32[:], in_=mask_bf[:])
 
-        gain_psum = psum_keep.tile([P, E], F32)
-        shift_psum = psum_keep.tile([P, E], F32)
-        for i in range(-5, N_CHUNKS + 1):
-            if i == -2:
-                nc.tensor.matmul(out=gain_psum[:], lhsT=ones[:], rhs=vector_rows[:, 0, :], start=True, stop=True)
-                nc.tensor.matmul(out=shift_psum[:], lhsT=ones[:], rhs=vector_rows[:, 1, :], start=True, stop=True)
-            for q in range(2):
-                for_plane(layer1_pass, i + 2, q)
-            when_in_range(negate_mean, i)
-            when_in_range(deviation, i)
-            when_in_range(regroup_on_vector, i + 1)
-            when_in_range(quantise_x, i + 3)
-            when_in_range(quantise_h, i + 1)
-            for_tile(shift_and_store, i - 1, 2)
-            for_tile(shift_and_store, i - 1, 3)
-            when_in_range(invert_std, i)
-            when_in_range(row_factors, i)
-            when_in_range(standardise, i)
-            for q in range(2):
-                for_tile(layer2_pass, i + 1, q)
-            when_in_range(open_sums, i + 1)
-            for_tile(add_bias, i + 1, 0)
-            for_plane(layer1_pass, i + 2, 2)
-            for_tile(layer2_pass, i + 1, 2)
-            for_tile(add_bias, i + 1, 1)
-            for_plane(layer1_pass, i + 2, 3)
-            for_tile(layer2_pass, i + 1, 3)
-            for_tile(add_bias, i + 1, 2)
-            for_tile(add_bias, i + 1, 3)
-            for_tile(gain_on_vector, i, 0)
-            for_tile(gain_on_vector, i, 1)
-            for_tile(shift_and_store, i, 0)
-            for_tile(shift_and_store, i, 1)
-            when_in_range(relu_h, i + 2)
-            when_in_range(group_h, i + 2)
-            for_tile(flip, i + 4, 0)
-            for_tile(flip, i + 4, 2)
-            for_tile(group_x, i + 4, 0)
-            for_tile(group_x, i + 4, 2)
-            when_in_range(load, i + 6)
+        def quantise_w3():
+            nc.vector.tensor_copy(out=w3_grouped[:], in_=w3_raw[:].rearrange("p t n -> p n t"))
+            nc.vector.quantize_mx(
+                out=w3_codes[:].bitcast(FP8X4),
+                scales=w3_scales[:],
+                in_=w3_grouped[:].rearrange("p n t -> p (n t)"),
+            )
+
+        gain_and_shift = psum_keep.tile([P, 2, E], BF16)
+        gain_psum = gain_and_shift[:, 0, :]
+        shift_psum = gain_and_shift[:, 1, :]
+        for c in range(2):
+            flip(c, 0)
+            flip(c, 2)
+            group_x(c, 0)
+            group_x(c, 2)
+        quantise_x(0)
+        layer1_pass(0, 0)
+        layer1_pass(0, 1)
+        quantise_w3()
+        for i in range(N_CHUNKS + 3):
+            when_in_range(relu_h1, i, 0)
+            when_in_range(layer1_pass, i, 2)
+            when_in_range(relu_h1, i, 1)
+            when_in_range(layer1_pass, i, 3)
+            when_in_range(relu_h1, i, 2)
+            when_in_range(relu_h1, i, 3)
+            when_in_range(group_h, i)
+            for_tile(add_bias, i - 1, 0)
+            for_tile(layer2_pass, i - 1, 2)
+            for_tile(add_bias, i - 1, 1)
+            for_tile(layer2_pass, i - 1, 3)
+            for_tile(shift_and_store, i - 2, 0)
+            for_tile(shift_pass, i - 2, 1)
+            for_tile(add_bias, i - 1, 2)
+            for_tile(add_bias, i - 1, 3)
+            for_tile(shift_and_store, i - 2, 1)
+            for_tile(shift_and_store, i - 3, 3)
+            if i == 1:
+                nc.tensor.matmul(out=gain_psum, lhsT=ones[:], rhs=vector_rows[:, 0, :], start=True, stop=True)
+                nc.tensor.matmul(out=shift_psum, lhsT=ones[:], rhs=vector_rows[:, 1, :], start=True, stop=True)
+            for_tile(flip, i + 2, 0)
+            for_tile(flip, i + 2, 2)
+            for_tile(shift_pass, i - 1, 0)
+            when_in_range(negate_mean, i - 1)
+            when_in_range(deviation, i - 1)
+            for_tile(group_x, i + 2, 0)
+            for_tile(group_x, i + 2, 2)
+            when_in_range(quantise_x, i + 1)
+            when_in_range(regroup_on_vector, i)
+            for_tile(shift_and_store, i - 2, 2)
+            when_in_range(quantise_h, i)
+            when_in_range(invert_std, i - 1)
+            when_in_range(row_factors, i - 1)
+            for_tile(gain_on_gpsimd, i - 1, 2)
+            for_tile(gain_on_gpsimd, i - 1, 3)
+            for_tile(gain_on_vector, i - 1, 0)
+            for_tile(gain_on_vector, i - 1, 1)
+            when_in_range(open_sums, i)
+            when_in_range(layer1_pass, i + 1, 0)
+            when_in_range(layer1_pass, i + 1, 1)
+            for_tile(layer2_pass, i, 0)
+            for_tile(layer2_pass, i, 1)
+            when_in_range(load, i + 4)

@@ -18,7 +18,6 @@ ROWS = 2 * 64 * 64
 ROWS_PER_PARTITION = ROWS // P
 WORDS = E // 2
 EPS = 1e-5
-VECTOR_COLUMNS = 256
 WIDTHS = [4] * 16
 N_CHUNKS = len(WIDTHS)
 FIRST = [sum(WIDTHS[:c]) for c in range(N_CHUNKS)]
@@ -37,7 +36,6 @@ def tile_edgefeaturenet_pb_t_kernel(tc, h1, edge_mask, W2, b2, W3, b3, ln_g, ln_
         two = ctx.enter_context(tc.tile_pool(name="two", bufs=2))
         three = ctx.enter_context(tc.tile_pool(name="three", bufs=3))
         four = ctx.enter_context(tc.tile_pool(name="four", bufs=4))
-        eight = ctx.enter_context(tc.tile_pool(name="eight", bufs=8))
         psum_t = ctx.enter_context(tc.psum_pool(name="psum_t", bufs=2))
         psum_1 = ctx.enter_context(tc.psum_pool(name="psum_1", bufs=2))
         psum_2 = ctx.enter_context(tc.psum_pool(name="psum_2", bufs=2))
@@ -100,7 +98,7 @@ def tile_edgefeaturenet_pb_t_kernel(tc, h1, edge_mask, W2, b2, W3, b3, ln_g, ln_
             )
             live["acc1", c, m] = acc1
 
-        def relu_h1(c, m):
+        def relu_h(c, m):
             if m == 0:
                 live["h_planes", c] = three.tile([P, PACK, WIDTHS[c] * P], BF16, name="h_planes")
             plane = live["h_planes", c][:, m, :]
@@ -111,7 +109,7 @@ def tile_edgefeaturenet_pb_t_kernel(tc, h1, edge_mask, W2, b2, W3, b3, ln_g, ln_
             h_planes = live["h_planes", c]
             h_grouped = three.tile([P, WIDTHS[c] * P, PACK], BF16, align_bytes=64, name="h_grouped")
             live["h_grouped", c] = h_grouped
-            regroup(nc.scalar.copy, c, 0, WIDTHS[c] * P - VECTOR_COLUMNS)
+            regroup(nc.scalar.copy, c, 0, WIDTHS[c] * P // 2)
 
         def regroup(copy, c, first, last):
             copy(
@@ -120,7 +118,7 @@ def tile_edgefeaturenet_pb_t_kernel(tc, h1, edge_mask, W2, b2, W3, b3, ln_g, ln_
             )
 
         def regroup_on_vector(c):
-            regroup(nc.vector.tensor_copy, c, WIDTHS[c] * P - VECTOR_COLUMNS, WIDTHS[c] * P)
+            regroup(nc.vector.tensor_copy, c, WIDTHS[c] * P // 2, WIDTHS[c] * P)
 
         def quantise_h(c):
             cols = WIDTHS[c] * P
@@ -167,28 +165,32 @@ def tile_edgefeaturenet_pb_t_kernel(tc, h1, edge_mask, W2, b2, W3, b3, ln_g, ln_
             nc.scalar.activation(out=neg_mean[:], in_=live["row_sum", c][:], func=ACT.Copy, scale=-1.0 / E)
             live["neg_mean", c] = neg_mean
 
-        def deviation(c):
+        def squares(c):
             square_sum = three.tile([P, WIDTHS[c]], F32, name="square_sum")
             for j in range(WIDTHS[c]):
-                squares = two.tile([P, E], F32, name="squares")
+                square = two.tile([P, E], F32, name="square")
                 nc.scalar.activation(
-                    out=squares[:],
+                    out=square[:],
                     in_=live["y", c][:, j, :],
                     func=ACT.Square,
                     bias=live["neg_mean", c][:, j : j + 1],
                     scale=1.0,
                     accum_out=square_sum[:, j : j + 1],
                 )
-            std = three.tile([P, WIDTHS[c]], F32, name="std")
-            nc.scalar.activation(out=std[:], in_=square_sum[:], func=ACT.Sqrt, bias=eps[:, 0:1], scale=1.0 / E)
-            live["std", c] = std
+            live["square_sum", c] = square_sum
 
         def invert_std(c):
             inv_std = three.tile([P, WIDTHS[c]], F32, name="inv_std")
-            nc.vector.reciprocal(out=inv_std[:], in_=live["std", c][:])
+            nc.scalar.activation(
+                out=inv_std[:],
+                in_=live["square_sum", c][:],
+                func=ACT.Abs_reciprocal_sqrt,
+                bias=eps[:, 0:1],
+                scale=1.0 / E,
+            )
             live["inv_std", c] = inv_std
 
-        def row_factors(c):
+        def mask_the_scale(c):
             row_scale = three.tile([P, WIDTHS[c]], F32, name="row_scale")
             nc.gpsimd.tensor_tensor(
                 out=row_scale[:],
@@ -196,24 +198,27 @@ def tile_edgefeaturenet_pb_t_kernel(tc, h1, edge_mask, W2, b2, W3, b3, ln_g, ln_
                 in1=mask_f32[:, FIRST[c] : FIRST[c] + WIDTHS[c]],
                 op=ALU.mult,
             )
-            row_offset = three.tile([P, WIDTHS[c]], F32, name="row_offset")
-            nc.gpsimd.tensor_tensor(out=row_offset[:], in0=live["neg_mean", c][:], in1=row_scale[:], op=ALU.mult)
             live["row_scale", c] = row_scale
-            live["row_offset", c] = row_offset
 
-        def gain_on_gpsimd(c, j):
-            standard = two.tile([P, E], F32, name="standard")
-            nc.gpsimd.tensor_scalar(
-                out=standard[:],
-                in0=live["y", c][:, j, :],
-                scalar1=live["row_scale", c][:, j : j + 1],
-                scalar2=live["row_offset", c][:, j : j + 1],
-                op0=ALU.mult,
-                op1=ALU.add,
+        def gain_on_gpsimd(c):
+            if not tile_is_gpsimds(WIDTHS[c] - 1):
+                return
+            standard = two.tile([P, 2, E], F32, name="standard")
+            for j in range(2):
+                nc.gpsimd.tensor_scalar(
+                    out=standard[:, j, :],
+                    in0=live["y", c][:, j + 2, :],
+                    scalar1=live["neg_mean", c][:, j + 2 : j + 3],
+                    scalar2=live["row_scale", c][:, j + 2 : j + 3],
+                    op0=ALU.add,
+                    op1=ALU.mult,
+                )
+            gained = three.tile([P, 2, E], F32, name="gpsimds_gained")
+            nc.gpsimd.tensor_tensor(
+                out=gained[:], in0=standard[:], in1=gain_all[:].unsqueeze(1).to_broadcast([P, 2, E]), op=ALU.mult
             )
-            gained = four.tile([P, E], F32, name="gpsimds_gained")
-            nc.gpsimd.tensor_tensor(out=gained[:], in0=standard[:], in1=gain_all[:], op=ALU.mult)
-            live["gained", c, j] = gained
+            for j in range(2):
+                live["gained", c, j + 2] = gained[:, j, :]
 
         def gain_on_vector(c, j):
             gained = four.tile([P, E], F32, name="gained")
@@ -225,7 +230,7 @@ def tile_edgefeaturenet_pb_t_kernel(tc, h1, edge_mask, W2, b2, W3, b3, ln_g, ln_
                 op0=ALU.add,
                 op1=ALU.mult,
             )
-            live["gained", c, j] = gained
+            live["gained", c, j] = gained[:]
 
         def shift_pass(c, j):
             masked_shift = psum_s.tile([P, E], F32, name="masked_shift")
@@ -244,14 +249,14 @@ def tile_edgefeaturenet_pb_t_kernel(tc, h1, edge_mask, W2, b2, W3, b3, ln_g, ln_
                     out=result[:, j, :],
                     in0=shift_psum,
                     scalar=mask_f32[:, t : t + 1],
-                    in1=live["gained", c, j][:],
+                    in1=live["gained", c, j],
                     op0=ALU.mult,
                     op1=ALU.add,
                 )
             else:
                 nc.vector.scalar_tensor_tensor(
                     out=result[:, j, :],
-                    in0=live["gained", c, j][:],
+                    in0=live["gained", c, j],
                     scalar=live["row_scale", c][:, j : j + 1],
                     in1=live["masked_shift", c, j][:],
                     op0=ALU.mult,
@@ -272,22 +277,18 @@ def tile_edgefeaturenet_pb_t_kernel(tc, h1, edge_mask, W2, b2, W3, b3, ln_g, ln_
             if 0 <= c < N_CHUNKS and j < WIDTHS[c]:
                 step(c, j)
 
-        def for_plane(step, c, m):
-            if 0 <= c < N_CHUNKS:
-                step(c, m)
-
         w2_raw = keep.tile([P, PACK, E], BF16)
         nc.sync.dma_start(out=w2_raw[:], in_=W2.rearrange("(q t) n -> q t n", t=PACK))
         load(0)
+        b2_bf = keep.tile([P, PACK], BF16)
+        nc.sync.dma_start(out=b2_bf[:], in_=b2.rearrange("(r m) -> r m", m=PACK))
+        mask_bf = keep.tile([P, ROWS_PER_PARTITION], BF16)
+        nc.sync.dma_start(out=mask_bf[:], in_=mask_rows)
         load(1)
         w3_raw = keep.tile([P, PACK, E], BF16)
         nc.sync.dma_start(out=w3_raw[:], in_=W3.rearrange("(p t) n -> p t n", t=PACK))
         load(2)
         load(3)
-        b2_bf = keep.tile([P, PACK], BF16)
-        nc.scalar.dma_start(out=b2_bf[:], in_=b2.rearrange("(r m) -> r m", m=PACK))
-        mask_bf = keep.tile([P, ROWS_PER_PARTITION], BF16)
-        nc.scalar.dma_start(out=mask_bf[:], in_=mask_rows)
         b3_all = keep.tile([P, E], BF16)
         nc.scalar.dma_start(out=b3_all[:], in_=b3.partition_broadcast(P))
         gain_all = keep.tile([P, E], BF16)
@@ -308,7 +309,7 @@ def tile_edgefeaturenet_pb_t_kernel(tc, h1, edge_mask, W2, b2, W3, b3, ln_g, ln_
         eps = keep.tile([P, 1], F32)
         nc.vector.memset(eps[:], EPS)
         table_warmer = keep.tile([P, 1], F32)
-        nc.scalar.activation(out=table_warmer[:], in_=eps[:], func=ACT.Sqrt)
+        nc.scalar.activation(out=table_warmer[:], in_=eps[:], func=ACT.Abs_reciprocal_sqrt)
 
         w2_grouped = keep.tile([P, E, PACK], BF16, align_bytes=64)
         nc.vector.tensor_copy(
@@ -325,16 +326,17 @@ def tile_edgefeaturenet_pb_t_kernel(tc, h1, edge_mask, W2, b2, W3, b3, ln_g, ln_
         mask_f32 = keep.tile([P, ROWS_PER_PARTITION], F32)
         nc.gpsimd.tensor_copy(out=mask_f32[:], in_=mask_bf[:])
         diagonals = keep.tile([P, 2 * N_CHUNKS, P], BF16)
-        for c in range(N_CHUNKS):
-            for j in range(2):
-                nc.gpsimd.tensor_scalar(
-                    out=diagonals[:, 2 * c + j, :],
-                    in0=ident_bf[:],
-                    scalar1=mask_f32[:, FIRST[c] + j : FIRST[c] + j + 1],
-                    scalar2=0.0,
-                    op0=ALU.mult,
-                    op1=ALU.add,
-                )
+
+        def mask_diagonals():
+            for c in range(N_CHUNKS):
+                for j in range(2):
+                    nc.vector.tensor_scalar(
+                        out=diagonals[:, 2 * c + j, :],
+                        in0=ident_bf[:],
+                        scalar1=mask_f32[:, FIRST[c] + j : FIRST[c] + j + 1],
+                        scalar2=None,
+                        op0=ALU.mult,
+                    )
 
         w3_grouped = keep.tile([P, E, PACK], BF16, align_bytes=64)
         w3_codes = keep.tile([P, E], U32, align_bytes=64)
@@ -351,22 +353,30 @@ def tile_edgefeaturenet_pb_t_kernel(tc, h1, edge_mask, W2, b2, W3, b3, ln_g, ln_
         gain_and_shift = psum_keep.tile([P, 2, E], BF16)
         gain_psum = gain_and_shift[:, 0, :]
         shift_psum = gain_and_shift[:, 1, :]
-        for c in range(2):
-            flip(c, 0)
-            flip(c, 2)
-            group_x(c, 0)
-            group_x(c, 2)
+        flip(0, 0)
+        flip(0, 2)
+        group_x(0, 0)
+        group_x(0, 2)
         quantise_x(0)
+        flip(1, 0)
+        group_x(1, 0)
         layer1_pass(0, 0)
         layer1_pass(0, 1)
+        flip(1, 2)
         quantise_w3()
-        for i in range(N_CHUNKS + 3):
-            when_in_range(relu_h1, i, 0)
+        mask_diagonals()
+        for i in range(N_CHUNKS + 2):
+            when_in_range(relu_h, i, 0)
             when_in_range(layer1_pass, i, 2)
-            when_in_range(relu_h1, i, 1)
+            when_in_range(relu_h, i, 1)
             when_in_range(layer1_pass, i, 3)
-            when_in_range(relu_h1, i, 2)
-            when_in_range(relu_h1, i, 3)
+            if i == 0:
+                flip(2, 0)
+                group_x(1, 2)
+                quantise_x(1)
+            when_in_range(relu_h, i, 2)
+            when_in_range(relu_h, i, 3)
+            for_tile(group_x, i + 2, 0)
             when_in_range(group_h, i)
             for_tile(add_bias, i - 1, 0)
             for_tile(layer2_pass, i - 1, 2)
@@ -377,25 +387,27 @@ def tile_edgefeaturenet_pb_t_kernel(tc, h1, edge_mask, W2, b2, W3, b3, ln_g, ln_
             for_tile(add_bias, i - 1, 2)
             for_tile(add_bias, i - 1, 3)
             for_tile(shift_and_store, i - 2, 1)
-            for_tile(shift_and_store, i - 3, 3)
+            if i - 3 < N_CHUNKS - 2:
+                for_tile(shift_and_store, i - 3, 3)
             if i == 1:
                 nc.tensor.matmul(out=gain_psum, lhsT=ones[:], rhs=vector_rows[:, 0, :], start=True, stop=True)
                 nc.tensor.matmul(out=shift_psum, lhsT=ones[:], rhs=vector_rows[:, 1, :], start=True, stop=True)
-            for_tile(flip, i + 2, 0)
             for_tile(flip, i + 2, 2)
             for_tile(shift_pass, i - 1, 0)
+            for_tile(flip, i + 3, 0)
             when_in_range(negate_mean, i - 1)
-            when_in_range(deviation, i - 1)
-            for_tile(group_x, i + 2, 0)
             for_tile(group_x, i + 2, 2)
-            when_in_range(quantise_x, i + 1)
+            when_in_range(squares, i - 1)
+            when_in_range(invert_std, i - 1)
+            when_in_range(mask_the_scale, i - 1)
+            when_in_range(gain_on_gpsimd, i - 1)
+            if i > 0:
+                when_in_range(quantise_x, i + 1)
             when_in_range(regroup_on_vector, i)
             for_tile(shift_and_store, i - 2, 2)
+            if N_CHUNKS - 2 <= i - 2 < N_CHUNKS:
+                shift_and_store(i - 2, 3)
             when_in_range(quantise_h, i)
-            when_in_range(invert_std, i - 1)
-            when_in_range(row_factors, i - 1)
-            for_tile(gain_on_gpsimd, i - 1, 2)
-            for_tile(gain_on_gpsimd, i - 1, 3)
             for_tile(gain_on_vector, i - 1, 0)
             for_tile(gain_on_vector, i - 1, 1)
             when_in_range(open_sums, i)

@@ -45,8 +45,8 @@ def tile_edgefeaturenet_pb_t_kernel(tc, h1, edge_mask, W2, b2, W3, b3, ln_g, ln_
 
         live = {}
 
-        def tile_is_gpsimds(j):
-            return j >= 2
+        def tile_is_gpsimds(c, j):
+            return j >= 2 and c < N_CHUNKS - 1
 
         def load(c):
             x = four.tile([P, WIDTHS[c] * E], BF16, name="x")
@@ -113,8 +113,8 @@ def tile_edgefeaturenet_pb_t_kernel(tc, h1, edge_mask, W2, b2, W3, b3, ln_g, ln_
 
         def regroup(copy, c, first, last):
             copy(
-                out=live["h_grouped", c][:, first:last, :].rearrange("p (n i) t -> p n t i", i=4),
-                in_=live["h_planes", c][:, :, first:last].rearrange("p t (n i) -> p n t i", i=4),
+                out=live["h_grouped", c][:, first:last, :],
+                in_=live["h_planes", c][:, :, first:last].rearrange("p t n -> p n t"),
             )
 
         def regroup_on_vector(c):
@@ -201,7 +201,7 @@ def tile_edgefeaturenet_pb_t_kernel(tc, h1, edge_mask, W2, b2, W3, b3, ln_g, ln_
             live["row_scale", c] = row_scale
 
         def gain_on_gpsimd(c):
-            if not tile_is_gpsimds(WIDTHS[c] - 1):
+            if not tile_is_gpsimds(c, WIDTHS[c] - 1):
                 return
             standard = two.tile([P, 2, E], F32, name="standard")
             for j in range(2):
@@ -233,7 +233,10 @@ def tile_edgefeaturenet_pb_t_kernel(tc, h1, edge_mask, W2, b2, W3, b3, ln_g, ln_
             live["gained", c, j] = gained[:]
 
         def shift_pass(c, j):
-            masked_shift = psum_s.tile([P, E], F32, name="masked_shift")
+            if c == N_CHUNKS - 1 and j > 0:
+                masked_shift = psum_1.tile([P, E], F32, name="acc1") if j == 1 else psum_t.tile([P, E], F32, name="flipped")
+            else:
+                masked_shift = psum_s.tile([P, E], F32, name="masked_shift")
             nc.tensor.matmul(
                 out=masked_shift[:], lhsT=diagonals[:, 2 * c + j, :], rhs=shift_all[:], start=True, stop=True
             )
@@ -244,7 +247,7 @@ def tile_edgefeaturenet_pb_t_kernel(tc, h1, edge_mask, W2, b2, W3, b3, ln_g, ln_
                 live["result", c] = three.tile([P, WIDTHS[c], E], F32, name="result")
             result = live["result", c]
             t = FIRST[c] + j
-            if tile_is_gpsimds(j):
+            if tile_is_gpsimds(c, j):
                 nc.vector.scalar_tensor_tensor(
                     out=result[:, j, :],
                     in0=shift_psum,
@@ -262,8 +265,8 @@ def tile_edgefeaturenet_pb_t_kernel(tc, h1, edge_mask, W2, b2, W3, b3, ln_g, ln_
                     op0=ALU.mult,
                     op1=ALU.add,
                 )
-            if j % 2 == 1:
-                first = j - 1
+            if j % 2 == 1 or c == N_CHUNKS - 1:
+                first = j - j % 2 if c < N_CHUNKS - 1 else j
                 nc.sync.dma_start(
                     out=out_rows[:, (FIRST[c] + first) * E : (FIRST[c] + j + 1) * E],
                     in_=result[:, first : j + 1, :].rearrange("p j f -> p (j f)"),
@@ -325,11 +328,11 @@ def tile_edgefeaturenet_pb_t_kernel(tc, h1, edge_mask, W2, b2, W3, b3, ln_g, ln_
         )
         mask_f32 = keep.tile([P, ROWS_PER_PARTITION], F32)
         nc.gpsimd.tensor_copy(out=mask_f32[:], in_=mask_bf[:])
-        diagonals = keep.tile([P, 2 * N_CHUNKS, P], BF16)
+        diagonals = keep.tile([P, 2 * N_CHUNKS + 2, P], BF16)
 
         def mask_diagonals():
             for c in range(N_CHUNKS):
-                for j in range(2):
+                for j in range(2 if c < N_CHUNKS - 1 else PACK):
                     nc.vector.tensor_scalar(
                         out=diagonals[:, 2 * c + j, :],
                         in0=ident_bf[:],
@@ -410,6 +413,10 @@ def tile_edgefeaturenet_pb_t_kernel(tc, h1, edge_mask, W2, b2, W3, b3, ln_g, ln_
             when_in_range(quantise_h, i)
             for_tile(gain_on_vector, i - 1, 0)
             for_tile(gain_on_vector, i - 1, 1)
+            if i == N_CHUNKS:
+                for j in range(2, PACK):
+                    shift_pass(i - 1, j)
+                    gain_on_vector(i - 1, j)
             when_in_range(open_sums, i)
             when_in_range(layer1_pass, i + 1, 0)
             when_in_range(layer1_pass, i + 1, 1)

@@ -113,8 +113,8 @@ def tile_edgefeaturenet_pb_t_kernel(tc, h1, edge_mask, W2, b2, W3, b3, ln_g, ln_
 
         def regroup(copy, c, first, last):
             copy(
-                out=live["h_grouped", c][:, first:last, :],
-                in_=live["h_planes", c][:, :, first:last].rearrange("p t n -> p n t"),
+                out=live["h_grouped", c][:, first:last, :].rearrange("p (n i) t -> p n t i", i=8),
+                in_=live["h_planes", c][:, :, first:last].rearrange("p t (n i) -> p n t i", i=8),
             )
 
         def regroup_on_vector(c):
@@ -281,8 +281,8 @@ def tile_edgefeaturenet_pb_t_kernel(tc, h1, edge_mask, W2, b2, W3, b3, ln_g, ln_
                 step(c, j)
 
         w2_raw = keep.tile([P, PACK, E], BF16)
-        nc.sync.dma_start(out=w2_raw[:], in_=W2.rearrange("(q t) n -> q t n", t=PACK))
         load(0)
+        nc.sync.dma_start(out=w2_raw[:], in_=W2.rearrange("(q t) n -> q t n", t=PACK))
         b2_bf = keep.tile([P, PACK], BF16)
         nc.sync.dma_start(out=b2_bf[:], in_=b2.rearrange("(r m) -> r m", m=PACK))
         mask_bf = keep.tile([P, ROWS_PER_PARTITION], BF16)

@@ -70,7 +70,8 @@ def tile_edgefeaturenet_pb_t_kernel(tc, h1, edge_mask, W2, b2, W3, b3, ln_g, ln_
                 live["x_grouped", c] = two.tile([P, WIDTHS[c] * E], BF16, align_bytes=64, name="x_grouped")
             x_grouped_words = live["x_grouped", c][:].bitcast(F32).rearrange("q (n u) -> q n u", u=2)
             n = min(2, WIDTHS[c] - first) * P
-            nc.scalar.copy(
+            copy = nc.vector.tensor_copy if c == 3 else nc.scalar.copy
+            copy(
                 out=x_grouped_words[:, first * P : first * P + n, :],
                 in_=live["flipped", c, first][:, :, 0:n].rearrange("q u n -> q n u"),
             )
@@ -192,24 +193,31 @@ def tile_edgefeaturenet_pb_t_kernel(tc, h1, edge_mask, W2, b2, W3, b3, ln_g, ln_
 
         def mask_the_scale(c):
             row_scale = three.tile([P, WIDTHS[c]], F32, name="row_scale")
-            nc.gpsimd.tensor_tensor(
-                out=row_scale[:],
-                in0=live["inv_std", c][:],
-                in1=mask_f32[:, FIRST[c] : FIRST[c] + WIDTHS[c]],
-                op=ALU.mult,
-            )
+            if c < N_CHUNKS - 1:
+                nc.gpsimd.tensor_tensor(
+                    out=row_scale[:],
+                    in0=live["inv_std", c][:],
+                    in1=mask_f32[:, FIRST[c] : FIRST[c] + WIDTHS[c]],
+                    op=ALU.mult,
+                )
+            else:
+                for j in range(PACK):
+                    nc.scalar.activation(
+                        out=row_scale[:, j : j + 1],
+                        in_=live["inv_std", c][:, j : j + 1],
+                        func=ACT.Copy,
+                        scale=mask_f32[:, FIRST[c] + j : FIRST[c] + j + 1],
+                    )
             live["row_scale", c] = row_scale
 
         def gain_on_gpsimd(c):
-            if not tile_is_gpsimds(c, WIDTHS[c] - 1):
-                return
             standard = two.tile([P, 2, E], F32, name="standard")
             for j in range(2):
                 nc.gpsimd.tensor_scalar(
                     out=standard[:, j, :],
                     in0=live["y", c][:, j + 2, :],
                     scalar1=live["neg_mean", c][:, j + 2 : j + 3],
-                    scalar2=live["row_scale", c][:, j + 2 : j + 3],
+                    scalar2=live["row_scale", c][:, j + 2 : j + 3] if c < N_CHUNKS - 1 else 1.0,
                     op0=ALU.add,
                     op1=ALU.mult,
                 )
@@ -416,7 +424,6 @@ def tile_edgefeaturenet_pb_t_kernel(tc, h1, edge_mask, W2, b2, W3, b3, ln_g, ln_
             if i == N_CHUNKS:
                 for j in range(2, PACK):
                     shift_pass(i - 1, j)
-                    gain_on_vector(i - 1, j)
             when_in_range(open_sums, i)
             when_in_range(layer1_pass, i + 1, 0)
             when_in_range(layer1_pass, i + 1, 1)

from contextlib import ExitStack

import concourse.mybir as mybir
from concourse.masks import make_identity

F32 = mybir.dt.float32
BF16 = mybir.dt.bfloat16
U32 = mybir.dt.uint32
U8 = mybir.dt.uint8
FP8X4 = mybir.dt.float8_e4m3fn_x4
ALU = mybir.AluOpType
ACT = mybir.ActivationFunctionType

P = 128
PACK = 4
E = 512
ROWS = 2 * 64 * 64
ROWS_PER_PARTITION = ROWS // P
WORDS = E // 2
EPS = 1e-5
WIDTHS = [4] * 16
N_CHUNKS = len(WIDTHS)
FIRST = [sum(WIDTHS[:c]) for c in range(N_CHUNKS)]

FLOPS = 2 * 2 * ROWS * E * E


def tile_edgefeaturenet_pb_t_kernel(tc, h1, edge_mask, W2, b2, W3, b3, ln_g, ln_b, out):
    nc = tc.nc
    h1_rows = h1.flatten_outer_dims().rearrange("(p t) k -> p (t k)", t=ROWS_PER_PARTITION)
    out_rows = out.flatten_outer_dims().rearrange("(p t) f -> p (t f)", t=ROWS_PER_PARTITION)
    mask_rows = edge_mask.rearrange("b n m -> (b n m)").rearrange("(p t) -> p t", t=ROWS_PER_PARTITION)

    with ExitStack() as ctx:
        keep = ctx.enter_context(tc.tile_pool(name="keep", bufs=1))
        two = ctx.enter_context(tc.tile_pool(name="two", bufs=2))
        three = ctx.enter_context(tc.tile_pool(name="three", bufs=3))
        four = ctx.enter_context(tc.tile_pool(name="four", bufs=4))
        psum_t = ctx.enter_context(tc.psum_pool(name="psum_t", bufs=2))
        psum_1 = ctx.enter_context(tc.psum_pool(name="psum_1", bufs=2))
        psum_2 = ctx.enter_context(tc.psum_pool(name="psum_2", bufs=2))
        psum_keep = ctx.enter_context(tc.psum_pool(name="psum_keep", bufs=1))
        psum_s = ctx.enter_context(tc.psum_pool(name="psum_s", bufs=1))
        ctx.enter_context(tc.manual_schedule())

        live = {}

        def tile_is_gpsimds(c, j):
            return j >= 2 and c < N_CHUNKS - 1

        def load(c):
            x = four.tile([P, WIDTHS[c] * E], BF16, name="x")
            nc.sync.dma_start(out=x[:], in_=h1_rows[:, FIRST[c] * E : (FIRST[c] + WIDTHS[c]) * E])
            live["x", c] = x

        def flip(c, first):
            x_words = live["x", c][:].bitcast(F32)
            flipped = psum_t.tile([P, 2, 2 * P], F32, name="flipped")
            for j in range(first, min(first + 2, WIDTHS[c])):
                for u in range(2):
                    nc.tensor.transpose(
                        flipped[:, u, (j - first) * P : (j - first + 1) * P],
                        x_words[:, j * WORDS + u : (j + 1) * WORDS : 2],
                        ident[:],
                    )
            live["flipped", c, first] = flipped

        def group_x(c, first):
            if first == 0:
                live["x_grouped", c] = two.tile([P, WIDTHS[c] * E], BF16, align_bytes=64, name="x_grouped")
            x_grouped_words = live["x_grouped", c][:].bitcast(F32).rearrange("q (n u) -> q n u", u=2)
            n = min(2, WIDTHS[c] - first) * P
            copy = nc.vector.tensor_copy if c == 3 else nc.scalar.copy
            copy(
                out=x_grouped_words[:, first * P : first * P + n, :],
                in_=live["flipped", c, first][:, :, 0:n].rearrange("q u n -> q n u"),
            )

        def quantise_x(c):
            cols = WIDTHS[c] * P
            x_codes = four.tile([P, cols], U32, align_bytes=64, name="x_codes")
            x_scales = four.tile([P, cols], U8, align_bytes=64, name="x_scales")
            nc.vector.quantize_mx(
                out=x_codes[:].bitcast(FP8X4), scales=x_scales[:], in_=live["x_grouped", c][:]
            )
            live["x_codes", c] = x_codes
            live["x_scales", c] = x_scales

        def layer1_pass(c, m):
            acc1 = psum_1.tile([P, WIDTHS[c] * P], F32, name="acc1")
            nc.tensor.matmul_mx(
                out=acc1[:],
                lhsT=w2_codes[:, m * P : (m + 1) * P].bitcast(FP8X4),
                lhsT_scale=w2_scales[:, m * P : (m + 1) * P],
                rhs=live["x_codes", c][:].bitcast(FP8X4),
                rhs_scale=live["x_scales", c][:],
                start=True,
                stop=True,
            )
            live["acc1", c, m] = acc1

        def relu_h(c, m):
            if m == 0:
                live["h_planes", c] = three.tile([P, PACK, WIDTHS[c] * P], BF16, name="h_planes")
            plane = live["h_planes", c][:, m, :]
            bias = b2_bf[:, m : m + 1]
            nc.scalar.activation(out=plane, in_=live["acc1", c, m][:], func=ACT.Relu, bias=bias, scale=1.0)

        def group_h(c):
            h_planes = live["h_planes", c]
            h_grouped = three.tile([P, WIDTHS[c] * P, PACK], BF16, align_bytes=64, name="h_grouped")
            live["h_grouped", c] = h_grouped
            regroup(nc.scalar.copy, c, 0, WIDTHS[c] * P // 2)

        def regroup(copy, c, first, last):
            copy(
                out=live["h_grouped", c][:, first:last, :].rearrange("p (n i) t -> p n t i", i=8),
                in_=live["h_planes", c][:, :, first:last].rearrange("p t (n i) -> p n t i", i=8),
            )

        def regroup_on_vector(c):
            regroup(nc.vector.tensor_copy, c, WIDTHS[c] * P // 2, WIDTHS[c] * P)

        def quantise_h(c):
            cols = WIDTHS[c] * P
            h_codes = three.tile([P, cols], U32, align_bytes=64, name="h_codes")
            h_scales = three.tile([P, cols], U8, align_bytes=64, name="h_scales")
            nc.vector.quantize_mx(
                out=h_codes[:].bitcast(FP8X4),
                scales=h_scales[:],
                in_=live["h_grouped", c][:].rearrange("p n t -> p (n t)"),
            )
            live["h_codes", c] = h_codes
            live["h_scales", c] = h_scales

        def layer2_pass(c, j):
            acc2 = psum_2.tile([P, E], F32, name="acc2")
            nc.tensor.matmul_mx(
                out=acc2[:],
                lhsT=live["h_codes", c][:, j * P : (j + 1) * P].bitcast(FP8X4),
                lhsT_scale=live["h_scales", c][:, j * P : (j + 1) * P],
                rhs=w3_codes[:].bitcast(FP8X4),
                rhs_scale=w3_scales[:],
                start=True,
                stop=True,
            )
            live["acc2", c, j] = acc2

        def open_sums(c):
            live["y", c] = three.tile([P, WIDTHS[c], E], F32, name="y")
            live["row_sum", c] = three.tile([P, WIDTHS[c]], F32, name="row_sum")

        def add_bias(c, j):
            nc.vector.scalar_tensor_tensor(
                out=live["y", c][:, j, :],
                in0=live["acc2", c, j][:],
                scalar=1.0,
                in1=b3_all[:],
                op0=ALU.mult,
                op1=ALU.add,
                accum_out=live["row_sum", c][:, j : j + 1],
            )

        def negate_mean(c):
            neg_mean = three.tile([P, WIDTHS[c]], F32, name="neg_mean")
            nc.scalar.activation(out=neg_mean[:], in_=live["row_sum", c][:], func=ACT.Copy, scale=-1.0 / E)
            live["neg_mean", c] = neg_mean

        def squares(c):
            square_sum = three.tile([P, WIDTHS[c]], F32, name="square_sum")
            for j in range(WIDTHS[c]):
                square = two.tile([P, E], F32, name="square")
                nc.scalar.activation(
                    out=square[:],
                    in_=live["y", c][:, j, :],
                    func=ACT.Square,
                    bias=live["neg_mean", c][:, j : j + 1],
                    scale=1.0,
                    accum_out=square_sum[:, j : j + 1],
                )
            live["square_sum", c] = square_sum

        def invert_std(c):
            inv_std = three.tile([P, WIDTHS[c]], F32, name="inv_std")
            nc.scalar.activation(
                out=inv_std[:],
                in_=live["square_sum", c][:],
                func=ACT.Abs_reciprocal_sqrt,
                bias=eps[:, 0:1],
                scale=1.0 / E,
            )
            live["inv_std", c] = inv_std

        def mask_the_scale(c):
            row_scale = three.tile([P, WIDTHS[c]], F32, name="row_scale")
            if c < N_CHUNKS - 1:
                nc.gpsimd.tensor_tensor(
                    out=row_scale[:],
                    in0=live["inv_std", c][:],
                    in1=mask_f32[:, FIRST[c] : FIRST[c] + WIDTHS[c]],
                    op=ALU.mult,
                )
            else:
                for j in range(PACK):
                    nc.scalar.activation(
                        out=row_scale[:, j : j + 1],
                        in_=live["inv_std", c][:, j : j + 1],
                        func=ACT.Copy,
                        scale=mask_f32[:, FIRST[c] + j : FIRST[c] + j + 1],
                    )
            live["row_scale", c] = row_scale

        def gain_on_gpsimd(c):
            standard = two.tile([P, 2, E], F32, name="standard")
            for j in range(2):
                nc.gpsimd.tensor_scalar(
                    out=standard[:, j, :],
                    in0=live["y", c][:, j + 2, :],
                    scalar1=live["neg_mean", c][:, j + 2 : j + 3],
                    scalar2=live["row_scale", c][:, j + 2 : j + 3] if c < N_CHUNKS - 1 else 1.0,
                    op0=ALU.add,
                    op1=ALU.mult,
                )
            gained = three.tile([P, 2, E], F32, name="gpsimds_gained")
            nc.gpsimd.tensor_tensor(
                out=gained[:], in0=standard[:], in1=gain_all[:].unsqueeze(1).to_broadcast([P, 2, E]), op=ALU.mult
            )
            for j in range(2):
                live["gained", c, j + 2] = gained[:, j, :]

        def gain_on_vector(c, j):
            gained = four.tile([P, E], F32, name="gained")
            nc.vector.scalar_tensor_tensor(
                out=gained[:],
                in0=live["y", c][:, j, :],
                scalar=live["neg_mean", c][:, j : j + 1],
                in1=gain_psum,
                op0=ALU.add,
                op1=ALU.mult,
            )
            live["gained", c, j] = gained[:]

        def shift_pass(c, j):
            if c == N_CHUNKS - 1 and j > 0:
                masked_shift = psum_1.tile([P, E], F32, name="acc1") if j == 1 else psum_t.tile([P, E], F32, name="flipped")
            else:
                masked_shift = psum_s.tile([P, E], F32, name="masked_shift")
            nc.tensor.matmul(
                out=masked_shift[:], lhsT=diagonals[:, 2 * c + j, :], rhs=shift_all[:], start=True, stop=True
            )
            live["masked_shift", c, j] = masked_shift

        def shift_and_store(c, j):
            if j == 0:
                live["result", c] = three.tile([P, WIDTHS[c], E], F32, name="result")
            result = live["result", c]
            t = FIRST[c] + j
            if tile_is_gpsimds(c, j):
                nc.vector.scalar_tensor_tensor(
                    out=result[:, j, :],
                    in0=shift_psum,
                    scalar=mask_f32[:, t : t + 1],
                    in1=live["gained", c, j],
                    op0=ALU.mult,
                    op1=ALU.add,
                )
            else:
                nc.vector.scalar_tensor_tensor(
                    out=result[:, j, :],
                    in0=live["gained", c, j],
                    scalar=live["row_scale", c][:, j : j + 1],
                    in1=live["masked_shift", c, j][:],
                    op0=ALU.mult,
                    op1=ALU.add,
                )
            if j % 2 == 1 or c == N_CHUNKS - 1:
                first = j - j % 2 if c < N_CHUNKS - 1 else j
                nc.sync.dma_start(
                    out=out_rows[:, (FIRST[c] + first) * E : (FIRST[c] + j + 1) * E],
                    in_=result[:, first : j + 1, :].rearrange("p j f -> p (j f)"),
                )

        def when_in_range(step, c, *rest):
            if 0 <= c < N_CHUNKS:
                step(c, *rest)

        def for_tile(step, c, j):
            if 0 <= c < N_CHUNKS and j < WIDTHS[c]:
                step(c, j)

        w2_raw = keep.tile([P, PACK, E], BF16)
        load(0)
        nc.sync.dma_start(out=w2_raw[:], in_=W2.rearrange("(q t) n -> q t n", t=PACK))
        b2_bf = keep.tile([P, PACK], BF16)
        nc.sync.dma_start(out=b2_bf[:], in_=b2.rearrange("(r m) -> r m", m=PACK))
        mask_bf = keep.tile([P, ROWS_PER_PARTITION], BF16)
        nc.sync.dma_start(out=mask_bf[:], in_=mask_rows)
        load(1)
        w3_raw = keep.tile([P, PACK, E], BF16)
        nc.sync.dma_start(out=w3_raw[:], in_=W3.rearrange("(p t) n -> p t n", t=PACK))
        load(2)
        load(3)
        b3_all = keep.tile([P, E], BF16)
        nc.scalar.dma_start(out=b3_all[:], in_=b3.partition_broadcast(P))
        gain_all = keep.tile([P, E], BF16)
        nc.scalar.dma_start(out=gain_all[:], in_=ln_g.partition_broadcast(P))
        shift_all = keep.tile([P, E], BF16)
        nc.scalar.dma_start(out=shift_all[:], in_=ln_b.partition_broadcast(P))
        ones = keep.tile([P, P], BF16)
        nc.vector.memset(ones[:], 1.0)
        vector_rows = keep.tile([P, 2, E], BF16)
        nc.vector.memset(vector_rows[:], 0.0)
        nc.scalar.dma_start(out=vector_rows[0:1, 0, :], in_=ln_g.rearrange("(o f) -> o f", o=1))
        nc.scalar.dma_start(out=vector_rows[0:1, 1, :], in_=ln_b.rearrange("(o f) -> o f", o=1))

        ident = keep.tile([P, P], F32)
        make_identity(nc, ident[:])
        ident_bf = keep.tile([P, P], BF16)
        make_identity(nc, ident_bf[:])
        eps = keep.tile([P, 1], F32)
        nc.vector.memset(eps[:], EPS)
        table_warmer = keep.tile([P, 1], F32)
        nc.scalar.activation(out=table_warmer[:], in_=eps[:], func=ACT.Abs_reciprocal_sqrt)

        w2_grouped = keep.tile([P, E, PACK], BF16, align_bytes=64)
        nc.vector.tensor_copy(
            out=w2_grouped[:].rearrange("q (m r) t -> q m r t", m=PACK),
            in_=w2_raw[:].rearrange("q t (r m) -> q m r t", m=PACK),
        )
        w2_codes = keep.tile([P, E], U32, align_bytes=64)
        w2_scales = keep.tile([P, E], U8, align_bytes=64)
        nc.vector.quantize_mx(
            out=w2_codes[:].bitcast(FP8X4),
            scales=w2_scales[:],
            in_=w2_grouped[:].rearrange("q n t -> q (n t)"),
        )
        mask_f32 = keep.tile([P, ROWS_PER_PARTITION], F32)
        nc.gpsimd.tensor_copy(out=mask_f32[:], in_=mask_bf[:])
        diagonals = keep.tile([P, 2 * N_CHUNKS + 2, P], BF16)

        def mask_diagonals():
            for c in range(N_CHUNKS):
                for j in range(2 if c < N_CHUNKS - 1 else PACK):
                    nc.vector.tensor_scalar(
                        out=diagonals[:, 2 * c + j, :],
                        in0=ident_bf[:],
                        scalar1=mask_f32[:, FIRST[c] + j : FIRST[c] + j + 1],
                        scalar2=None,
                        op0=ALU.mult,
                    )

        w3_grouped = keep.tile([P, E, PACK], BF16, align_bytes=64)
        w3_codes = keep.tile([P, E], U32, align_bytes=64)
        w3_scales = keep.tile([P, E], U8, align_bytes=64)

        def quantise_w3():
            nc.vector.tensor_copy(out=w3_grouped[:], in_=w3_raw[:].rearrange("p t n -> p n t"))
            nc.vector.quantize_mx(
                out=w3_codes[:].bitcast(FP8X4),
                scales=w3_scales[:],
                in_=w3_grouped[:].rearrange("p n t -> p (n t)"),
            )

        gain_and_shift = psum_keep.tile([P, 2, E], BF16)
        gain_psum = gain_and_shift[:, 0, :]
        shift_psum = gain_and_shift[:, 1, :]
        flip(0, 0)
        flip(0, 2)
        group_x(0, 0)
        group_x(0, 2)
        quantise_x(0)
        flip(1, 0)
        group_x(1, 0)
        layer1_pass(0, 0)
        layer1_pass(0, 1)
        flip(1, 2)
        quantise_w3()
        mask_diagonals()
        for i in range(N_CHUNKS + 2):
            when_in_range(relu_h, i, 0)
            when_in_range(layer1_pass, i, 2)
            when_in_range(relu_h, i, 1)
            when_in_range(layer1_pass, i, 3)
            if i == 0:
                flip(2, 0)
                group_x(1, 2)
                quantise_x(1)
            when_in_range(relu_h, i, 2)
            when_in_range(relu_h, i, 3)
            for_tile(group_x, i + 2, 0)
            when_in_range(group_h, i)
            for_tile(add_bias, i - 1, 0)
            for_tile(layer2_pass, i - 1, 2)
            for_tile(add_bias, i - 1, 1)
            for_tile(layer2_pass, i - 1, 3)
            for_tile(shift_and_store, i - 2, 0)
            for_tile(shift_pass, i - 2, 1)
            for_tile(add_bias, i - 1, 2)
            for_tile(add_bias, i - 1, 3)
            for_tile(shift_and_store, i - 2, 1)
            if i - 3 < N_CHUNKS - 2:
                for_tile(shift_and_store, i - 3, 3)
            if i == 1:
                nc.tensor.matmul(out=gain_psum, lhsT=ones[:], rhs=vector_rows[:, 0, :], start=True, stop=True)
                nc.tensor.matmul(out=shift_psum, lhsT=ones[:], rhs=vector_rows[:, 1, :], start=True, stop=True)
            for_tile(flip, i + 2, 2)
            for_tile(shift_pass, i - 1, 0)
            for_tile(flip, i + 3, 0)
            when_in_range(negate_mean, i - 1)
            for_tile(group_x, i + 2, 2)
            when_in_range(squares, i - 1)
            when_in_range(invert_std, i - 1)
            when_in_range(mask_the_scale, i - 1)
            when_in_range(gain_on_gpsimd, i - 1)
            if i > 0:
                when_in_range(quantise_x, i + 1)
            when_in_range(regroup_on_vector, i)
            for_tile(shift_and_store, i - 2, 2)
            if N_CHUNKS - 2 <= i - 2 < N_CHUNKS:
                shift_and_store(i - 2, 3)
            when_in_range(quantise_h, i)
            for_tile(gain_on_vector, i - 1, 0)
            for_tile(gain_on_vector, i - 1, 1)
            if i == N_CHUNKS:
                for j in range(2, PACK):
                    shift_pass(i - 1, j)
            when_in_range(open_sums, i)
            when_in_range(layer1_pass, i + 1, 0)
            when_in_range(layer1_pass, i + 1, 1)
            for_tile(layer2_pass, i, 0)
            for_tile(layer2_pass, i, 1)
            when_in_range(load, i + 4)
